import numpy as np
import ml_dtypes


def mxq(x, axis, fmt="e4m3"):
    dtype, down = {"e4m3": (ml_dtypes.float8_e4m3fn, 7), "e5m2": (ml_dtypes.float8_e5m2, 14)}[fmt]
    v = np.moveaxis(np.asarray(x, np.float32).astype(ml_dtypes.bfloat16).astype(np.float64), axis, -1)
    blocks = v.reshape(v.shape[:-1] + (-1, 32))
    amax = np.abs(blocks).max(-1, keepdims=True)
    byte = np.maximum(np.where(amax > 0, np.frexp(amax)[1] - 1 + 127, 0) - down, 1)
    scale = np.exp2(byte - 127.0)
    codes = (blocks / scale).astype(np.float32).astype(dtype).astype(np.float64)
    return np.moveaxis((codes * scale).reshape(v.shape), -1, axis)


WIDE = False


def mx_kscale(k):
    if not WIDE:
        return np.ones(k)
    levels = np.array([10, -10, 5, -5, 0])
    a = np.random.permutation(np.resize(levels, k // 512 * 4)).reshape(k // 512, 4)
    idx = np.arange(k)
    return np.exp2(a[idx // 512, idx % 128 // 32])


BF16 = ml_dtypes.bfloat16


def bf(x):
    return np.asarray(x, np.float32).astype(BF16)


def f64(x):
    return np.asarray(x).astype(np.float64)


B, N, D, F, O = 64, 4, 512, 512, 384
NEG = -1e9


def erf(v):
    a = np.clip(v, -6.0, 6.0)
    a2 = 2.0 * a * a
    top = a2.max()
    term, tot, r, n = a.copy(), a.copy(), 1.0, 0
    while r > 1e-18:
        n += 1
        r *= top / (2 * n + 1)
        term *= a2
        term /= 2 * n + 1
        tot += term
    return 2.0 / np.sqrt(np.pi) * np.exp(-a * a) * tot


def gelu(v):
    return 0.5 * v * (1.0 + erf(v / np.sqrt(2.0)))


def setup_inputs():
    s = mx_kscale(D)
    return {"x": bf(np.random.standard_normal((B, N, D)) * s),
            "W1": bf(np.random.standard_normal((2 * D, F)) / np.sqrt(2 * D) / np.tile(s, 2)[:, None]),
            "b1": bf(np.random.standard_normal(F) * 0.2),
            "W2": bf(np.random.standard_normal((F, O)) / np.sqrt(F)),
            "b2": bf(np.random.standard_normal(O) * 0.2)}


def reference(x, W1, b1, W2, b2):
    xq = mxq(f64(x), 2, "e4m3")
    W1 = f64(W1)
    ai = xq @ mxq(W1[:D], 0, "e4m3")
    aj = xq @ mxq(W1[D:], 0, "e4m3")
    ii, jj = np.tril_indices(N)
    h = gelu(ai[:, ii, :] + aj[:, jj, :] + f64(b1))
    pu = (mxq(h, 2, "e4m3") @ mxq(f64(W2), 0, "e4m3")) + f64(b2)
    p = np.zeros((B, N, N, O))
    p[:, ii, jj, :] = pu
    mask = np.triu(np.ones((N, N), dtype=bool), 1)
    sq = np.sum(p * p, axis=-1)
    s = np.sqrt(np.where(mask[None], 1.0, sq))
    s = np.where(mask[None], NEG, s)
    e = np.exp(s - s.max(-1, keepdims=True))
    w = e / e.sum(-1, keepdims=True)
    return np.sum(w[..., None] * p, axis=2)

@@ -1,0 +1,311 @@
+from contextlib import ExitStack
+
+import concourse.masks as masks
+import concourse.mybir as mybir
+
+F32 = mybir.dt.float32
+BF16 = mybir.dt.bfloat16
+U32 = mybir.dt.uint32
+U8 = mybir.dt.uint8
+FP8X4 = mybir.dt.float8_e4m3fn_x4
+ACT = mybir.ActivationFunctionType
+ALU = mybir.AluOpType
+AXIS = mybir.AxisListType
+
+BATCH, POSITIONS, D, F, O = 64, 4, 512, 512, 384
+P = 128
+PACK = 4
+HALF = 64
+NEG = -1e9
+
+FLOPS = 2 * BATCH * POSITIONS * 2 * D * F + 2 * BATCH * 10 * F * O
+
+PAIRS = (
+    ((2, 0), (3, 1)),
+    ((2, 1), (3, 2)),
+    ((2, 2), (3, 3)),
+    ((1, 0), (3, 0)),
+    ((1, 1), (0, 0)),
+)
+TILES = len(PAIRS)
+ROWS_OF_RESULT = ((2, 3), (1, 0))
+BLOCK_ORDER = (1, 0, 0, 1, 2, 3, 1, 3)
+X_COLS = len(BLOCK_ORDER) * HALF
+
+W1_VECTOR_COLS = 80
+PRE_AHEAD = 2
+
+
+def first_block(low, high):
+    for block in range(len(BLOCK_ORDER) - 1):
+        if BLOCK_ORDER[block] == low and BLOCK_ORDER[block + 1] == high:
+            return block
+    raise ValueError("BLOCK_ORDER lacks a pair of positions")
+
+
+def tile_pairconnect_s_kernel(tc, x, W1, b1, W2, b2, out):
+    nc = tc.nc
+    with ExitStack() as ctx:
+        keep = ctx.enter_context(tc.tile_pool(name="keep", bufs=1))
+        work = ctx.enter_context(tc.tile_pool(name="work", bufs=2))
+        psum_once = ctx.enter_context(tc.psum_pool(name="psum_once", bufs=1))
+        psum_pre = ctx.enter_context(tc.psum_pool(name="psum_pre", bufs=PRE_AHEAD + 1))
+        psum_q = ctx.enter_context(tc.psum_pool(name="psum_q", bufs=3))
+        ctx.enter_context(tc.manual_schedule())
+
+        b2_row = keep.tile([P, O], BF16)
+        nc.vector.memset(b2_row[:], 0.0)
+        nc.scalar.dma_start(out=b2_row[0:1, :], in_=b2.unsqueeze(0))
+        b1_bf = keep.tile([P, PACK], BF16)
+        nc.scalar.dma_start(out=b1_bf[:], in_=b1.rearrange("(q t) -> q t", t=PACK))
+
+        x_rows = keep.tile([P, 2 * D], BF16)
+        nc.sync.dma_start(
+            out=x_rows[:].rearrange("r (g k) -> r g k", g=2),
+            in_=x.flatten_outer_dims().rearrange("(g r) k -> r g k", r=P),
+        )
+        w1_rows = keep.tile([P, 2, PACK, F], BF16)
+        for half in range(2):
+            nc.sync.dma_start(
+                out=w1_rows[:, half],
+                in_=W1[half * D : (half + 1) * D, :].rearrange("(p j) f -> p j f", j=PACK),
+            )
+        w2_rows = keep.tile([P, PACK, O], BF16)
+        nc.sync.dma_start(out=w2_rows[:], in_=W2.rearrange("(p j) o -> p j o", j=PACK))
+
+        zero = keep.tile([P, 1], F32)
+        nc.vector.memset(zero[:], 0.0)
+        warm = keep.tile([P, 1], F32)
+        nc.scalar.activation(out=warm[:], in_=zero[:], func=ACT.Gelu)
+
+        ones = keep.tile([P, P], BF16)
+        nc.vector.memset(ones[:], 1.0)
+        ident = keep.tile([P, P], F32)
+        masks.make_identity(nc, ident[:])
+        member = keep.tile([P, 2, TILES], F32)
+        nc.gpsimd.memset(member[:], NEG)
+        for m in range(TILES):
+            for side in range(2):
+                for a in range(2):
+                    if ROWS_OF_RESULT[a][side] == PAIRS[m][side][0]:
+                        rows = slice(side * HALF, (side + 1) * HALF)
+                        nc.gpsimd.memset(member[rows, a, m : m + 1], 0.0)
+
+        b2_ps = psum_once.tile([P, O], F32)
+        nc.tensor.matmul(out=b2_ps[:], lhsT=ones[:], rhs=b2_row[:], start=True, stop=True)
+        b2_all = keep.tile([P, O], F32)
+        nc.scalar.copy(out=b2_all[:], in_=b2_ps[:])
+        b1_f32 = keep.tile([P, PACK], F32)
+        nc.vector.tensor_copy(out=b1_f32[:], in_=b1_bf[:])
+
+        x_words = x_rows[:].bitcast(F32).rearrange("r (g p u) -> r g u p", g=2, u=2)
+        x_t = psum_once.tile([P, 2, 2 * P], F32)
+        for g in range(2):
+            for u in range(2):
+                nc.tensor.transpose(
+                    out=x_t[:, u, g * P : (g + 1) * P], in_=x_words[:, g, u, :], identity=ident[:]
+                )
+        x_grouped = keep.tile([P, X_COLS * PACK], BF16, align_bytes=64)
+        x_grouped_words = x_grouped[:].bitcast(F32).rearrange(
+            "p (s b u) -> p s b u", s=len(BLOCK_ORDER), u=2
+        )
+        x_t_by_position = x_t[:].rearrange("p u (b i) -> p i b u", i=POSITIONS)
+        for block in range(len(BLOCK_ORDER)):
+            nc.scalar.copy(
+                out=x_grouped_words[:, block], in_=x_t_by_position[:, BLOCK_ORDER[block]]
+            )
+        x_codes = keep.tile([P, X_COLS], U32, align_bytes=64)
+        x_scales = keep.tile([P, X_COLS], U8, align_bytes=64)
+
+        w1_grouped = keep.tile([P, 2 * PACK * F], BF16, align_bytes=64)
+        w1_grouped_view = w1_grouped[:].rearrange(
+            "p (h t q j) -> p h t q j", h=2, t=PACK, j=PACK
+        )
+        w1_codes = keep.tile([P, 2 * F], U32, align_bytes=64)
+        w1_scales = keep.tile([P, 2 * F], U8, align_bytes=64)
+
+        def regroup_w1(copy, half, cols):
+            copy(
+                out=w1_grouped_view[:, half, :, cols, :].rearrange("p t q j -> p q j t"),
+                in_=w1_rows[:, half].rearrange("p j (q t) -> p q j t", t=PACK)[:, cols],
+            )
+
+        def quantise_w1(half):
+            nc.vector.quantize_mx(
+                out=w1_codes[:, half * F : (half + 1) * F].bitcast(FP8X4),
+                scales=w1_scales[:, half * F : (half + 1) * F],
+                in_=w1_grouped[:, half * PACK * F : (half + 1) * PACK * F],
+            )
+
+        vector_cols = slice(0, W1_VECTOR_COLS)
+        scalar_cols = slice(W1_VECTOR_COLS, P)
+        regroup_w1(nc.vector.tensor_copy, 0, vector_cols)
+        regroup_w1(nc.scalar.copy, 0, scalar_cols)
+        nc.vector.quantize_mx(
+            out=x_codes[:].bitcast(FP8X4), scales=x_scales[:], in_=x_grouped[:]
+        )
+        regroup_w1(nc.vector.tensor_copy, 1, vector_cols)
+        regroup_w1(nc.scalar.copy, 1, scalar_cols)
+        quantise_w1(0)
+        quantise_w1(1)
+
+        w2_grouped = keep.tile([P, O, PACK], BF16, align_bytes=64)
+        nc.scalar.copy(
+            out=w2_grouped[:].rearrange("p (c i) j -> p c j i", i=4),
+            in_=w2_rows[:].rearrange("p j (c i) -> p c j i", i=4),
+        )
+        w2_codes = keep.tile([P, O], U32, align_bytes=64)
+        w2_scales = keep.tile([P, O], U8, align_bytes=64)
+        w2_parts = ((0, 256), (256, 384))
+
+        def quantise_w2():
+            flat = w2_grouped[:].rearrange("p o j -> p (o j)")
+            for lo, hi in w2_parts:
+                nc.vector.quantize_mx(
+                    out=w2_codes[:, lo:hi].bitcast(FP8X4),
+                    scales=w2_scales[:, lo:hi],
+                    in_=flat[:, lo * PACK : hi * PACK],
+                )
+
+        h_codes = keep.tile([P, TILES, P], U32, align_bytes=64)
+        h_scales = keep.tile([P, TILES, P], U8, align_bytes=64)
+        p_all = keep.tile([P, TILES, O], F32)
+        p_squared = keep.tile([P, TILES, O], F32)
+        norm2 = keep.tile([P, TILES], F32)
+        pre_tiles = {}
+        h_tiles = {}
+        q_tiles = {}
+
+        def stage1(m):
+            (i_low, j_low), (i_high, j_high) = PAIRS[m]
+            pre = psum_pre.tile([P, PACK, P], F32, name="pre")
+            pre_tiles[m] = pre
+            starts = (first_block(i_low, i_high) * HALF, first_block(j_low, j_high) * HALF)
+            for t in range(PACK):
+                for half in range(2):
+                    w_cols = slice((half * PACK + t) * P, (half * PACK + t + 1) * P)
+                    x_cols = slice(starts[half], starts[half] + P)
+                    nc.tensor.matmul_mx(
+                        out=pre[:, t, :],
+                        lhsT=w1_codes[:, w_cols].bitcast(FP8X4),
+                        lhsT_scale=w1_scales[:, w_cols],
+                        rhs=x_codes[:, x_cols].bitcast(FP8X4),
+                        rhs_scale=x_scales[:, x_cols],
+                        start=(half == 0),
+                        stop=(half == 1),
+                    )
+
+        def add_b1_and_gelu(m):
+            v = work.tile([P, P, PACK], F32, name="v")
+            nc.vector.tensor_tensor(
+                out=v[:],
+                in0=pre_tiles[m][:].rearrange("q t w -> q w t"),
+                in1=b1_f32[:].unsqueeze(1).to_broadcast([P, P, PACK]),
+                op=ALU.add,
+            )
+            h = work.tile([P, P * PACK], BF16, name="h", align_bytes=64)
+            h_tiles[m] = h
+            nc.scalar.activation(out=h[:], in_=v[:].rearrange("q w t -> q (w t)"), func=ACT.Gelu)
+
+        def quantise_h_and_stage2(m):
+            nc.vector.quantize_mx(
+                out=h_codes[:, m, :].bitcast(FP8X4), scales=h_scales[:, m, :], in_=h_tiles[m][:]
+            )
+            q = psum_q.tile([P, O], F32, name="q")
+            q_tiles[m] = q
+            for lo, hi in w2_parts:
+                nc.tensor.matmul_mx(
+                    out=q[:, lo:hi],
+                    lhsT=h_codes[:, m, :].bitcast(FP8X4),
+                    lhsT_scale=h_scales[:, m, :],
+                    rhs=w2_codes[:, lo:hi].bitcast(FP8X4),
+                    rhs_scale=w2_scales[:, lo:hi],
+                    start=True,
+                    stop=True,
+                )
+
+        def add_b2_and_norm(m):
+            nc.vector.tensor_tensor(
+                out=p_all[:, m, :], in0=q_tiles[m][:], in1=b2_all[:], op=ALU.add
+            )
+            nc.scalar.activation(
+                out=p_squared[:, m, :],
+                in_=p_all[:, m, :],
+                func=ACT.Square,
+                accum_out=norm2[:, m : m + 1],
+            )
+
+        for m in range(PRE_AHEAD):
+            stage1(m)
+        for step in range(TILES + 2):
+            if step + PRE_AHEAD < TILES:
+                stage1(step + PRE_AHEAD)
+            if step < TILES:
+                add_b1_and_gelu(step)
+            if step == 0:
+                quantise_w2()
+            if 1 <= step <= TILES:
+                quantise_h_and_stage2(step - 1)
+            if step >= 2:
+                add_b2_and_norm(step - 2)
+
+        norm = keep.tile([P, TILES], F32)
+        nc.scalar.activation(out=norm[:], in_=norm2[:], func=ACT.Sqrt)
+        shape = [P, 2, TILES]
+        masked = keep.tile(shape, F32)
+        nc.vector.tensor_tensor(
+            out=masked[:], in0=norm[:].unsqueeze(1).to_broadcast(shape), in1=member[:], op=ALU.add
+        )
+        largest = keep.tile([P, 2], F32)
+        nc.vector.tensor_reduce(out=largest[:], in_=masked[:], axis=AXIS.X, op=ALU.max)
+        shifted = keep.tile(shape, F32)
+        nc.vector.tensor_tensor(
+            out=shifted[:],
+            in0=masked[:],
+            in1=largest[:].unsqueeze(2).to_broadcast(shape),
+            op=ALU.subtract,
+        )
+        expd = keep.tile(shape, F32)
+        nc.scalar.activation(out=expd[:], in_=shifted[:], func=ACT.Exp)
+        total = keep.tile([P, 2], F32)
+        nc.vector.tensor_reduce(out=total[:], in_=expd[:], axis=AXIS.X, op=ALU.add)
+        inverse = keep.tile([P, 2], F32)
+        nc.vector.reciprocal(out=inverse[:], in_=total[:])
+        weight = keep.tile(shape, F32)
+        nc.vector.tensor_tensor(
+            out=weight[:],
+            in0=expd[:],
+            in1=inverse[:].unsqueeze(2).to_broadcast(shape),
+            op=ALU.mult,
+        )
+
+        out_by_row = out.rearrange("b i o -> i b o")
+        results = {}
+        tiles_of = {}
+        for a in range(2):
+            tiles_of[a] = [
+                m
+                for m in range(TILES)
+                if any(ROWS_OF_RESULT[a][side] == PAIRS[m][side][0] for side in range(2))
+            ]
+            results[a] = keep.tile([P, O], F32, name="result%d" % a)
+            first = tiles_of[a][0]
+            nc.scalar.activation(
+                out=results[a][:],
+                in_=p_all[:, first, :],
+                func=ACT.Copy,
+                scale=weight[:, a, first : first + 1],
+            )
+        for a in (1, 0):
+            for m in tiles_of[a][1:]:
+                nc.vector.scalar_tensor_tensor(
+                    out=results[a][:],
+                    in0=p_all[:, m, :],
+                    scalar=weight[:, a, m : m + 1],
+                    in1=results[a][:],
+                    op0=ALU.mult,
+                    op1=ALU.add,
+                )
+            for side in range(2):
+                rows = slice(side * HALF, (side + 1) * HALF)
+                nc.sync.dma_start(out=out_by_row[ROWS_OF_RESULT[a][side]], in_=results[a][rows, :])

@@ -30,6 +30,7 @@ PAIRS = (
 TILES = len(PAIRS)
 ROWS_OF_RESULT = ((2, 3), (1, 0))
 BLOCK_ORDER = (1, 0, 0, 1, 2, 3, 1, 3)
+RUN_AT = 2
 X_COLS = len(BLOCK_ORDER) * HALF
 
 W1_VECTOR_COLS = 80
@@ -91,12 +92,8 @@ def tile_pairconnect_s_kernel(tc, x, W1, b1, W2, b2, out):
                         rows = slice(side * HALF, (side + 1) * HALF)
                         nc.gpsimd.memset(member[rows, a, m : m + 1], 0.0)
 
-        b2_ps = psum_once.tile([P, O], F32)
-        nc.tensor.matmul(out=b2_ps[:], lhsT=ones[:], rhs=b2_row[:], start=True, stop=True)
-        b2_all = keep.tile([P, O], F32)
-        nc.scalar.copy(out=b2_all[:], in_=b2_ps[:])
-        b1_f32 = keep.tile([P, PACK], F32)
-        nc.vector.tensor_copy(out=b1_f32[:], in_=b1_bf[:])
+        half_power = keep.tile([P, 1], F32)
+        nc.gpsimd.memset(half_power[:], 0.5)
 
         x_words = x_rows[:].bitcast(F32).rearrange("r (g p u) -> r g u p", g=2, u=2)
         x_t = psum_once.tile([P, 2, 2 * P], F32)
@@ -110,12 +107,29 @@ def tile_pairconnect_s_kernel(tc, x, W1, b1, W2, b2, out):
             "p (s b u) -> p s b u", s=len(BLOCK_ORDER), u=2
         )
         x_t_by_position = x_t[:].rearrange("p u (b i) -> p i b u", i=POSITIONS)
-        for block in range(len(BLOCK_ORDER)):
-            nc.scalar.copy(
-                out=x_grouped_words[:, block], in_=x_t_by_position[:, BLOCK_ORDER[block]]
-            )
         x_codes = keep.tile([P, X_COLS], U32, align_bytes=64)
         x_scales = keep.tile([P, X_COLS], U8, align_bytes=64)
+
+        def quantise_x(first, blocks):
+            cols = slice(first * HALF, (first + blocks) * HALF)
+            nc.vector.quantize_mx(
+                out=x_codes[:, cols].bitcast(FP8X4),
+                scales=x_scales[:, cols],
+                in_=x_grouped[:, first * HALF * PACK : (first + blocks) * HALF * PACK],
+            )
+
+        nc.vector.tensor_copy(
+            out=x_grouped_words[:, RUN_AT : RUN_AT + POSITIONS], in_=x_t_by_position
+        )
+        quantise_x(RUN_AT, POSITIONS)
+        for block in range(len(BLOCK_ORDER)):
+            if not RUN_AT <= block < RUN_AT + POSITIONS:
+                nc.scalar.copy(
+                    out=x_grouped_words[:, block], in_=x_t_by_position[:, BLOCK_ORDER[block]]
+                )
+
+        b2_ps = psum_once.tile([P, O], F32)
+        nc.tensor.matmul(out=b2_ps[:], lhsT=ones[:], rhs=b2_row[:], start=True, stop=True)
 
         w1_grouped = keep.tile([P, 2 * PACK * F], BF16, align_bytes=64)
         w1_grouped_view = w1_grouped[:].rearrange(
@@ -141,19 +155,22 @@ def tile_pairconnect_s_kernel(tc, x, W1, b1, W2, b2, out):
         scalar_cols = slice(W1_VECTOR_COLS, P)
         regroup_w1(nc.vector.tensor_copy, 0, vector_cols)
         regroup_w1(nc.scalar.copy, 0, scalar_cols)
-        nc.vector.quantize_mx(
-            out=x_codes[:].bitcast(FP8X4), scales=x_scales[:], in_=x_grouped[:]
-        )
+        quantise_x(0, RUN_AT)
+        quantise_x(RUN_AT + POSITIONS, len(BLOCK_ORDER) - RUN_AT - POSITIONS)
         regroup_w1(nc.vector.tensor_copy, 1, vector_cols)
         regroup_w1(nc.scalar.copy, 1, scalar_cols)
         quantise_w1(0)
         quantise_w1(1)
+        b1_f32 = keep.tile([P, PACK], F32)
+        nc.vector.tensor_copy(out=b1_f32[:], in_=b1_bf[:])
 
         w2_grouped = keep.tile([P, O, PACK], BF16, align_bytes=64)
         nc.scalar.copy(
             out=w2_grouped[:].rearrange("p (c i) j -> p c j i", i=4),
             in_=w2_rows[:].rearrange("p j (c i) -> p c j i", i=4),
         )
+        b2_all = keep.tile([P, O], F32)
+        nc.scalar.copy(out=b2_all[:], in_=b2_ps[:])
         w2_codes = keep.tile([P, O], U32, align_bytes=64)
         w2_scales = keep.tile([P, O], U8, align_bytes=64)
         w2_parts = ((0, 256), (256, 384))
@@ -172,6 +189,7 @@ def tile_pairconnect_s_kernel(tc, x, W1, b1, W2, b2, out):
         p_all = keep.tile([P, TILES, O], F32)
         p_squared = keep.tile([P, TILES, O], F32)
         norm2 = keep.tile([P, TILES], F32)
+        norm = keep.tile([P, TILES], F32)
         pre_tiles = {}
         h_tiles = {}
         q_tiles = {}
@@ -234,6 +252,9 @@ def tile_pairconnect_s_kernel(tc, x, W1, b1, W2, b2, out):
                 func=ACT.Square,
                 accum_out=norm2[:, m : m + 1],
             )
+            nc.gpsimd.tensor_tensor(
+                out=norm[:, m : m + 1], in0=norm2[:, m : m + 1], in1=half_power[:], op=ALU.pow
+            )
 
         for m in range(PRE_AHEAD):
             stage1(m)
@@ -249,8 +270,6 @@ def tile_pairconnect_s_kernel(tc, x, W1, b1, W2, b2, out):
             if step >= 2:
                 add_b2_and_norm(step - 2)
 
-        norm = keep.tile([P, TILES], F32)
-        nc.scalar.activation(out=norm[:], in_=norm2[:], func=ACT.Sqrt)
         shape = [P, 2, TILES]
         masked = keep.tile(shape, F32)
         nc.vector.tensor_tensor(
@@ -265,8 +284,17 @@ def tile_pairconnect_s_kernel(tc, x, W1, b1, W2, b2, out):
             in1=largest[:].unsqueeze(2).to_broadcast(shape),
             op=ALU.subtract,
         )
+        tanh = keep.tile(shape, F32)
+        nc.scalar.activation(out=tanh[:], in_=shifted[:], func=ACT.Tanh, scale=0.5)
+        denominator = keep.tile(shape, F32)
+        nc.vector.tensor_scalar(
+            out=denominator[:], in0=tanh[:], scalar1=-1.0, scalar2=1.0, op0=ALU.mult, op1=ALU.add
+        )
+        nc.vector.reciprocal(out=denominator[:], in_=denominator[:])
         expd = keep.tile(shape, F32)
-        nc.scalar.activation(out=expd[:], in_=shifted[:], func=ACT.Exp)
+        nc.vector.scalar_tensor_tensor(
+            out=expd[:], in0=tanh[:], scalar=1.0, in1=denominator[:], op0=ALU.add, op1=ALU.mult
+        )
         total = keep.tile([P, 2], F32)
         nc.vector.tensor_reduce(out=total[:], in_=expd[:], axis=AXIS.X, op=ALU.add)
         inverse = keep.tile([P, 2], F32)

@@ -35,6 +35,7 @@ X_COLS = len(BLOCK_ORDER) * HALF
 
 W1_VECTOR_COLS = 80
 PRE_AHEAD = 2
+CHAIN_LAG = 2
 
 
 def first_block(low, high):
@@ -42,6 +43,18 @@ def first_block(low, high):
         if BLOCK_ORDER[block] == low and BLOCK_ORDER[block + 1] == high:
             return block
     raise ValueError("BLOCK_ORDER lacks a pair of positions")
+
+
+def result_of(m, side):
+    for a in range(2):
+        if ROWS_OF_RESULT[a][side] == PAIRS[m][side][0]:
+            return a
+    raise ValueError("ROWS_OF_RESULT lacks an output row")
+
+
+def tiles_of_result(a):
+    tiles = [m for m in range(TILES) if a in (result_of(m, 0), result_of(m, 1))]
+    return tiles[0], tiles[-1] + 1
 
 
 def tile_pairconnect_s_kernel(tc, x, W1, b1, W2, b2, out):
@@ -83,15 +96,8 @@ def tile_pairconnect_s_kernel(tc, x, W1, b1, W2, b2, out):
         nc.vector.memset(ones[:], 1.0)
         ident = keep.tile([P, P], F32)
         masks.make_identity(nc, ident[:])
-        member = keep.tile([P, 2, TILES], F32)
-        nc.gpsimd.memset(member[:], NEG)
-        for m in range(TILES):
-            for side in range(2):
-                for a in range(2):
-                    if ROWS_OF_RESULT[a][side] == PAIRS[m][side][0]:
-                        rows = slice(side * HALF, (side + 1) * HALF)
-                        nc.gpsimd.memset(member[rows, a, m : m + 1], 0.0)
-
+        half_norm = keep.tile([P, 2, TILES], F32)
+        nc.gpsimd.memset(half_norm[:], NEG)
         half_power = keep.tile([P, 1], F32)
         nc.gpsimd.memset(half_power[:], 0.5)
 
@@ -188,8 +194,7 @@ def tile_pairconnect_s_kernel(tc, x, W1, b1, W2, b2, out):
         h_scales = keep.tile([P, TILES, P], U8, align_bytes=64)
         p_all = keep.tile([P, TILES, O], F32)
         p_squared = keep.tile([P, TILES, O], F32)
-        norm2 = keep.tile([P, TILES], F32)
-        norm = keep.tile([P, TILES], F32)
+        quarter_norm2 = keep.tile([P, TILES], F32)
         pre_tiles = {}
         h_tiles = {}
         q_tiles = {}
@@ -250,11 +255,19 @@ def tile_pairconnect_s_kernel(tc, x, W1, b1, W2, b2, out):
                 out=p_squared[:, m, :],
                 in_=p_all[:, m, :],
                 func=ACT.Square,
-                accum_out=norm2[:, m : m + 1],
+                scale=0.5,
+                accum_out=quarter_norm2[:, m : m + 1],
             )
-            nc.gpsimd.tensor_tensor(
-                out=norm[:, m : m + 1], in0=norm2[:, m : m + 1], in1=half_power[:], op=ALU.pow
-            )
+            for a in range(2):
+                sides = [side for side in range(2) if result_of(m, side) == a]
+                if sides:
+                    rows = slice(sides[0] * HALF, (sides[-1] + 1) * HALF)
+                    nc.gpsimd.tensor_tensor(
+                        out=half_norm[rows, a, m : m + 1],
+                        in0=quarter_norm2[rows, m : m + 1],
+                        in1=half_power[rows, :],
+                        op=ALU.pow,
+                    )
 
         for m in range(PRE_AHEAD):
             stage1(m)
@@ -271,69 +284,107 @@ def tile_pairconnect_s_kernel(tc, x, W1, b1, W2, b2, out):
                 add_b2_and_norm(step - 2)
 
         shape = [P, 2, TILES]
-        masked = keep.tile(shape, F32)
-        nc.vector.tensor_tensor(
-            out=masked[:], in0=norm[:].unsqueeze(1).to_broadcast(shape), in1=member[:], op=ALU.add
-        )
-        largest = keep.tile([P, 2], F32)
-        nc.vector.tensor_reduce(out=largest[:], in_=masked[:], axis=AXIS.X, op=ALU.max)
-        shifted = keep.tile(shape, F32)
-        nc.vector.tensor_tensor(
-            out=shifted[:],
-            in0=masked[:],
-            in1=largest[:].unsqueeze(2).to_broadcast(shape),
-            op=ALU.subtract,
-        )
+        neg_largest = keep.tile([P, 2], F32)
         tanh = keep.tile(shape, F32)
-        nc.scalar.activation(out=tanh[:], in_=shifted[:], func=ACT.Tanh, scale=0.5)
         denominator = keep.tile(shape, F32)
-        nc.vector.tensor_scalar(
-            out=denominator[:], in0=tanh[:], scalar1=-1.0, scalar2=1.0, op0=ALU.mult, op1=ALU.add
-        )
-        nc.vector.reciprocal(out=denominator[:], in_=denominator[:])
         expd = keep.tile(shape, F32)
-        nc.vector.scalar_tensor_tensor(
-            out=expd[:], in0=tanh[:], scalar=1.0, in1=denominator[:], op0=ALU.add, op1=ALU.mult
-        )
         total = keep.tile([P, 2], F32)
-        nc.vector.tensor_reduce(out=total[:], in_=expd[:], axis=AXIS.X, op=ALU.add)
         inverse = keep.tile([P, 2], F32)
-        nc.vector.reciprocal(out=inverse[:], in_=total[:])
         weight = keep.tile(shape, F32)
-        nc.vector.tensor_tensor(
-            out=weight[:],
-            in0=expd[:],
-            in1=inverse[:].unsqueeze(2).to_broadcast(shape),
-            op=ALU.mult,
+
+        def of(tile_, a):
+            lo, hi = tiles_of_result(a)
+            return tile_[:, a, lo:hi]
+
+        def shift_and_tanh(a):
+            nc.vector.tensor_reduce(
+                out=neg_largest[:, a : a + 1],
+                in_=of(half_norm, a),
+                axis=AXIS.X,
+                op=ALU.max,
+                negate=True,
+            )
+            nc.scalar.activation(
+                out=of(tanh, a), in_=of(half_norm, a), func=ACT.Tanh, bias=neg_largest[:, a : a + 1]
+            )
+
+        def one_minus_tanh(a):
+            nc.vector.tensor_scalar(
+                out=of(denominator, a),
+                in0=of(tanh, a),
+                scalar1=-1.0,
+                scalar2=1.0,
+                op0=ALU.mult,
+                op1=ALU.add,
+            )
+
+        def invert_denominator(a):
+            nc.vector.reciprocal(out=of(denominator, a), in_=of(denominator, a))
+
+        def exp_and_total(a):
+            nc.vector.scalar_tensor_tensor(
+                out=of(expd, a),
+                in0=of(tanh, a),
+                scalar=1.0,
+                in1=of(denominator, a),
+                op0=ALU.add,
+                op1=ALU.mult,
+                accum_out=total[:, a : a + 1],
+            )
+
+        def invert_total(a):
+            nc.vector.reciprocal(out=inverse[:, a : a + 1], in_=total[:, a : a + 1])
+
+        def normalise(a):
+            nc.vector.tensor_scalar(
+                out=of(weight, a),
+                in0=of(expd, a),
+                scalar1=inverse[:, a : a + 1],
+                scalar2=None,
+                op0=ALU.mult,
+            )
+
+        chain = (
+            shift_and_tanh,
+            one_minus_tanh,
+            invert_denominator,
+            exp_and_total,
+            invert_total,
+            normalise,
         )
+        for link in range(len(chain) + CHAIN_LAG):
+            if link < len(chain):
+                chain[link](0)
+            if link >= CHAIN_LAG:
+                chain[link - CHAIN_LAG](1)
 
         out_by_row = out.rearrange("b i o -> i b o")
         results = {}
-        tiles_of = {}
         for a in range(2):
-            tiles_of[a] = [
-                m
-                for m in range(TILES)
-                if any(ROWS_OF_RESULT[a][side] == PAIRS[m][side][0] for side in range(2))
-            ]
+            first = tiles_of_result(a)[0]
             results[a] = keep.tile([P, O], F32, name="result%d" % a)
-            first = tiles_of[a][0]
             nc.scalar.activation(
                 out=results[a][:],
                 in_=p_all[:, first, :],
                 func=ACT.Copy,
                 scale=weight[:, a, first : first + 1],
             )
-        for a in (1, 0):
-            for m in tiles_of[a][1:]:
-                nc.vector.scalar_tensor_tensor(
-                    out=results[a][:],
-                    in0=p_all[:, m, :],
-                    scalar=weight[:, a, m : m + 1],
-                    in1=results[a][:],
-                    op0=ALU.mult,
-                    op1=ALU.add,
-                )
-            for side in range(2):
-                rows = slice(side * HALF, (side + 1) * HALF)
-                nc.sync.dma_start(out=out_by_row[ROWS_OF_RESULT[a][side]], in_=results[a][rows, :])
+        for term in range(1, TILES):
+            for a in range(2):
+                lo, hi = tiles_of_result(a)
+                m = lo + term
+                if m < hi:
+                    nc.vector.scalar_tensor_tensor(
+                        out=results[a][:],
+                        in0=p_all[:, m, :],
+                        scalar=weight[:, a, m : m + 1],
+                        in1=results[a][:],
+                        op0=ALU.mult,
+                        op1=ALU.add,
+                    )
+                if m == hi - 1:
+                    for side in range(2):
+                        rows = slice(side * HALF, (side + 1) * HALF)
+                        nc.sync.dma_start(
+                            out=out_by_row[ROWS_OF_RESULT[a][side]], in_=results[a][rows, :]
+                        )

@@ -29,13 +29,13 @@ PAIRS = (
 )
 TILES = len(PAIRS)
 ROWS_OF_RESULT = ((2, 3), (1, 0))
+LONG, SHORT = 0, 1
 BLOCK_ORDER = (1, 0, 0, 1, 2, 3, 1, 3)
 RUN_AT = 2
 X_COLS = len(BLOCK_ORDER) * HALF
 
 W1_VECTOR_COLS = 80
 PRE_AHEAD = 2
-CHAIN_LAG = 2
 
 
 def first_block(low, high):
@@ -151,22 +151,24 @@ def tile_pairconnect_s_kernel(tc, x, W1, b1, W2, b2, out):
             )
 
         def quantise_w1(half):
-            nc.vector.quantize_mx(
-                out=w1_codes[:, half * F : (half + 1) * F].bitcast(FP8X4),
-                scales=w1_scales[:, half * F : (half + 1) * F],
-                in_=w1_grouped[:, half * PACK * F : (half + 1) * PACK * F],
-            )
+            for part in range(2 * half, 2 * half + 2):
+                cols = slice(part * F // 2, (part + 1) * F // 2)
+                nc.vector.quantize_mx(
+                    out=w1_codes[:, cols].bitcast(FP8X4),
+                    scales=w1_scales[:, cols],
+                    in_=w1_grouped[:, part * PACK * F // 2 : (part + 1) * PACK * F // 2],
+                )
 
         vector_cols = slice(0, W1_VECTOR_COLS)
         scalar_cols = slice(W1_VECTOR_COLS, P)
         regroup_w1(nc.vector.tensor_copy, 0, vector_cols)
         regroup_w1(nc.scalar.copy, 0, scalar_cols)
-        quantise_x(0, RUN_AT)
-        quantise_x(RUN_AT + POSITIONS, len(BLOCK_ORDER) - RUN_AT - POSITIONS)
         regroup_w1(nc.vector.tensor_copy, 1, vector_cols)
         regroup_w1(nc.scalar.copy, 1, scalar_cols)
         quantise_w1(0)
         quantise_w1(1)
+        quantise_x(0, RUN_AT)
+        quantise_x(RUN_AT + POSITIONS, len(BLOCK_ORDER) - RUN_AT - POSITIONS)
         b1_f32 = keep.tile([P, PACK], F32)
         nc.vector.tensor_copy(out=b1_f32[:], in_=b1_bf[:])
 
@@ -176,7 +178,6 @@ def tile_pairconnect_s_kernel(tc, x, W1, b1, W2, b2, out):
             in_=w2_rows[:].rearrange("p j (c i) -> p c j i", i=4),
         )
         b2_all = keep.tile([P, O], F32)
-        nc.scalar.copy(out=b2_all[:], in_=b2_ps[:])
         w2_codes = keep.tile([P, O], U32, align_bytes=64)
         w2_scales = keep.tile([P, O], U8, align_bytes=64)
         w2_parts = ((0, 256), (256, 384))
@@ -278,113 +279,91 @@ def tile_pairconnect_s_kernel(tc, x, W1, b1, W2, b2, out):
                 add_b1_and_gelu(step)
             if step == 0:
                 quantise_w2()
+                nc.scalar.copy(out=b2_all[:], in_=b2_ps[:])
             if 1 <= step <= TILES:
                 quantise_h_and_stage2(step - 1)
             if step >= 2:
                 add_b2_and_norm(step - 2)
 
-        shape = [P, 2, TILES]
-        neg_largest = keep.tile([P, 2], F32)
-        tanh = keep.tile(shape, F32)
-        denominator = keep.tile(shape, F32)
-        expd = keep.tile(shape, F32)
-        total = keep.tile([P, 2], F32)
-        inverse = keep.tile([P, 2], F32)
-        weight = keep.tile(shape, F32)
+        out_by_row = out.rearrange("b i o -> i b o")
 
-        def of(tile_, a):
-            lo, hi = tiles_of_result(a)
-            return tile_[:, a, lo:hi]
+        def store(a, result):
+            for side in range(2):
+                rows = slice(side * HALF, (side + 1) * HALF)
+                nc.sync.dma_start(out=out_by_row[ROWS_OF_RESULT[a][side]], in_=result[rows, :])
 
-        def shift_and_tanh(a):
-            nc.vector.tensor_reduce(
-                out=neg_largest[:, a : a + 1],
-                in_=of(half_norm, a),
-                axis=AXIS.X,
-                op=ALU.max,
-                negate=True,
-            )
-            nc.scalar.activation(
-                out=of(tanh, a), in_=of(half_norm, a), func=ACT.Tanh, bias=neg_largest[:, a : a + 1]
-            )
+        first, last = tiles_of_result(SHORT)[0], tiles_of_result(SHORT)[1] - 1
+        assert last == first + 1
+        difference = keep.tile([P, O], F32)
+        nc.vector.tensor_tensor(
+            out=difference[:], in0=p_all[:, last, :], in1=p_all[:, first, :], op=ALU.subtract
+        )
 
-        def one_minus_tanh(a):
-            nc.vector.tensor_scalar(
-                out=of(denominator, a),
-                in0=of(tanh, a),
-                scalar1=-1.0,
-                scalar2=1.0,
+        lo, hi = tiles_of_result(LONG)
+        neg_largest = keep.tile([P, 1], F32)
+        nc.vector.tensor_reduce(
+            out=neg_largest[:], in_=half_norm[:, LONG, lo:hi], axis=AXIS.X, op=ALU.max, negate=True
+        )
+        tanh = keep.tile([P, hi - lo], F32)
+        nc.scalar.activation(
+            out=tanh[:], in_=half_norm[:, LONG, lo:hi], func=ACT.Tanh, bias=neg_largest[:]
+        )
+        tanh_short = keep.tile([P, 1], F32)
+        nc.scalar.activation(
+            out=tanh_short[:],
+            in_=half_norm[:, SHORT, first : first + 1],
+            func=ACT.Tanh,
+            scale=-1.0,
+            bias=half_norm[:, SHORT, last : last + 1],
+        )
+        denominator = keep.tile([P, hi - lo], F32)
+        nc.vector.tensor_scalar(
+            out=denominator[:], in0=tanh[:], scalar1=-1.0, scalar2=1.0, op0=ALU.mult, op1=ALU.add
+        )
+        nc.vector.reciprocal(out=denominator[:], in_=denominator[:])
+        expd = keep.tile([P, hi - lo], F32)
+        total = keep.tile([P, 1], F32)
+        nc.vector.scalar_tensor_tensor(
+            out=expd[:],
+            in0=tanh[:],
+            scalar=1.0,
+            in1=denominator[:],
+            op0=ALU.add,
+            op1=ALU.mult,
+            accum_out=total[:],
+        )
+        inverse = keep.tile([P, 1], F32)
+        nc.vector.reciprocal(out=inverse[:], in_=total[:])
+        weight = keep.tile([P, hi - lo], F32)
+        nc.vector.tensor_scalar(
+            out=weight[:], in0=expd[:], scalar1=inverse[:], scalar2=None, op0=ALU.mult
+        )
+
+        long_result = keep.tile([P, O], F32)
+        nc.scalar.activation(
+            out=long_result[:], in_=p_all[:, lo, :], func=ACT.Copy, scale=weight[:, 0:1]
+        )
+        weight_last = keep.tile([P, 1], F32)
+        nc.vector.tensor_scalar(
+            out=weight_last[:], in0=tanh_short[:], scalar1=0.5, scalar2=0.5, op0=ALU.mult, op1=ALU.add
+        )
+        short_result = keep.tile([P, O], F32)
+        nc.vector.scalar_tensor_tensor(
+            out=short_result[:],
+            in0=difference[:],
+            scalar=weight_last[:],
+            in1=p_all[:, first, :],
+            op0=ALU.mult,
+            op1=ALU.add,
+        )
+        store(SHORT, short_result)
+        for m in range(lo + 1, hi):
+            nc.vector.scalar_tensor_tensor(
+                out=long_result[:],
+                in0=p_all[:, m, :],
+                scalar=weight[:, m - lo : m - lo + 1],
+                in1=long_result[:],
                 op0=ALU.mult,
                 op1=ALU.add,
             )
-
-        def invert_denominator(a):
-            nc.vector.reciprocal(out=of(denominator, a), in_=of(denominator, a))
-
-        def exp_and_total(a):
-            nc.vector.scalar_tensor_tensor(
-                out=of(expd, a),
-                in0=of(tanh, a),
-                scalar=1.0,
-                in1=of(denominator, a),
-                op0=ALU.add,
-                op1=ALU.mult,
-                accum_out=total[:, a : a + 1],
-            )
-
-        def invert_total(a):
-            nc.vector.reciprocal(out=inverse[:, a : a + 1], in_=total[:, a : a + 1])
-
-        def normalise(a):
-            nc.vector.tensor_scalar(
-                out=of(weight, a),
-                in0=of(expd, a),
-                scalar1=inverse[:, a : a + 1],
-                scalar2=None,
-                op0=ALU.mult,
-            )
-
-        chain = (
-            shift_and_tanh,
-            one_minus_tanh,
-            invert_denominator,
-            exp_and_total,
-            invert_total,
-            normalise,
-        )
-        for link in range(len(chain) + CHAIN_LAG):
-            if link < len(chain):
-                chain[link](0)
-            if link >= CHAIN_LAG:
-                chain[link - CHAIN_LAG](1)
-
-        out_by_row = out.rearrange("b i o -> i b o")
-        results = {}
-        for a in range(2):
-            first = tiles_of_result(a)[0]
-            results[a] = keep.tile([P, O], F32, name="result%d" % a)
-            nc.scalar.activation(
-                out=results[a][:],
-                in_=p_all[:, first, :],
-                func=ACT.Copy,
-                scale=weight[:, a, first : first + 1],
-            )
-        for term in range(1, TILES):
-            for a in range(2):
-                lo, hi = tiles_of_result(a)
-                m = lo + term
-                if m < hi:
-                    nc.vector.scalar_tensor_tensor(
-                        out=results[a][:],
-                        in0=p_all[:, m, :],
-                        scalar=weight[:, a, m : m + 1],
-                        in1=results[a][:],
-                        op0=ALU.mult,
-                        op1=ALU.add,
-                    )
-                if m == hi - 1:
-                    for side in range(2):
-                        rows = slice(side * HALF, (side + 1) * HALF)
-                        nc.sync.dma_start(
-                            out=out_by_row[ROWS_OF_RESULT[a][side]], in_=results[a][rows, :]
-                        )
+        store(LONG, long_result)

@@ -124,10 +124,7 @@ def tile_pairconnect_s_kernel(tc, x, W1, b1, W2, b2, out):
                 in_=x_grouped[:, first * HALF * PACK : (first + blocks) * HALF * PACK],
             )
 
-        nc.vector.tensor_copy(
-            out=x_grouped_words[:, RUN_AT : RUN_AT + POSITIONS], in_=x_t_by_position
-        )
-        quantise_x(RUN_AT, POSITIONS)
+        nc.scalar.copy(out=x_grouped_words[:, RUN_AT : RUN_AT + POSITIONS], in_=x_t_by_position)
         for block in range(len(BLOCK_ORDER)):
             if not RUN_AT <= block < RUN_AT + POSITIONS:
                 nc.scalar.copy(
@@ -163,6 +160,7 @@ def tile_pairconnect_s_kernel(tc, x, W1, b1, W2, b2, out):
         scalar_cols = slice(W1_VECTOR_COLS, P)
         regroup_w1(nc.vector.tensor_copy, 0, vector_cols)
         regroup_w1(nc.scalar.copy, 0, scalar_cols)
+        quantise_x(RUN_AT, POSITIONS)
         regroup_w1(nc.vector.tensor_copy, 1, vector_cols)
         regroup_w1(nc.scalar.copy, 1, scalar_cols)
         quantise_w1(0)

@@ -35,7 +35,8 @@ RUN_AT = 2
 X_COLS = len(BLOCK_ORDER) * HALF
 
 W1_VECTOR_COLS = 80
-PRE_AHEAD = 2
+Q_BANKS = (2, 4, 5, 6, 7)
+PRE_AHEAD = 3
 
 
 def first_block(low, high):
@@ -61,10 +62,7 @@ def tile_pairconnect_s_kernel(tc, x, W1, b1, W2, b2, out):
     nc = tc.nc
     with ExitStack() as ctx:
         keep = ctx.enter_context(tc.tile_pool(name="keep", bufs=1))
-        work = ctx.enter_context(tc.tile_pool(name="work", bufs=2))
-        psum_once = ctx.enter_context(tc.psum_pool(name="psum_once", bufs=1))
-        psum_pre = ctx.enter_context(tc.psum_pool(name="psum_pre", bufs=PRE_AHEAD + 1))
-        psum_q = ctx.enter_context(tc.psum_pool(name="psum_q", bufs=3))
+        banks = ctx.enter_context(tc.psum_pool(name="banks", bufs=1))
         ctx.enter_context(tc.manual_schedule())
 
         b2_row = keep.tile([P, O], BF16)
@@ -96,23 +94,28 @@ def tile_pairconnect_s_kernel(tc, x, W1, b1, W2, b2, out):
         nc.vector.memset(ones[:], 1.0)
         ident = keep.tile([P, P], F32)
         masks.make_identity(nc, ident[:])
-        half_norm = keep.tile([P, 2, TILES], F32)
-        nc.gpsimd.memset(half_norm[:], NEG)
-        half_power = keep.tile([P, 1], F32)
+        half_power = keep.tile([P, TILES], F32)
         nc.gpsimd.memset(half_power[:], 0.5)
+        long_bias = keep.tile([P, 1], F32)
+        nc.gpsimd.memset(long_bias[:], NEG)
+        short_bias = keep.tile([P, 1], F32)
+        nc.gpsimd.memset(short_bias[:], -NEG)
 
         x_words = x_rows[:].bitcast(F32).rearrange("r (g p u) -> r g u p", g=2, u=2)
-        x_t = psum_once.tile([P, 2, 2 * P], F32)
+        x_t = []
         for g in range(2):
+            x_t.append(banks.tile([P, 2, P], F32, name="bank%d" % g))
             for u in range(2):
                 nc.tensor.transpose(
-                    out=x_t[:, u, g * P : (g + 1) * P], in_=x_words[:, g, u, :], identity=ident[:]
+                    out=x_t[g][:, u, :], in_=x_words[:, g, u, :], identity=ident[:]
                 )
         x_grouped = keep.tile([P, X_COLS * PACK], BF16, align_bytes=64)
         x_grouped_words = x_grouped[:].bitcast(F32).rearrange(
-            "p (s b u) -> p s b u", s=len(BLOCK_ORDER), u=2
+            "p (s g b u) -> p g s b u", s=len(BLOCK_ORDER), g=2, u=2
         )
-        x_t_by_position = x_t[:].rearrange("p u (b i) -> p i b u", i=POSITIONS)
+        x_t_by_position = [
+            tile[:].rearrange("p u (b i) -> p i b u", i=POSITIONS) for tile in x_t
+        ]
         x_codes = keep.tile([P, X_COLS], U32, align_bytes=64)
         x_scales = keep.tile([P, X_COLS], U8, align_bytes=64)
 
@@ -124,14 +127,7 @@ def tile_pairconnect_s_kernel(tc, x, W1, b1, W2, b2, out):
                 in_=x_grouped[:, first * HALF * PACK : (first + blocks) * HALF * PACK],
             )
 
-        nc.scalar.copy(out=x_grouped_words[:, RUN_AT : RUN_AT + POSITIONS], in_=x_t_by_position)
-        for block in range(len(BLOCK_ORDER)):
-            if not RUN_AT <= block < RUN_AT + POSITIONS:
-                nc.scalar.copy(
-                    out=x_grouped_words[:, block], in_=x_t_by_position[:, BLOCK_ORDER[block]]
-                )
-
-        b2_ps = psum_once.tile([P, O], F32)
+        b2_ps = banks.tile([P, O], F32, name="bank2")
         nc.tensor.matmul(out=b2_ps[:], lhsT=ones[:], rhs=b2_row[:], start=True, stop=True)
 
         w1_grouped = keep.tile([P, 2 * PACK * F], BF16, align_bytes=64)
@@ -158,6 +154,9 @@ def tile_pairconnect_s_kernel(tc, x, W1, b1, W2, b2, out):
 
         vector_cols = slice(0, W1_VECTOR_COLS)
         scalar_cols = slice(W1_VECTOR_COLS, P)
+        run = slice(RUN_AT, RUN_AT + POSITIONS)
+        nc.vector.tensor_copy(out=x_grouped_words[:, 0, run], in_=x_t_by_position[0])
+        nc.scalar.copy(out=x_grouped_words[:, 1, run], in_=x_t_by_position[1])
         regroup_w1(nc.vector.tensor_copy, 0, vector_cols)
         regroup_w1(nc.scalar.copy, 0, scalar_cols)
         quantise_x(RUN_AT, POSITIONS)
@@ -165,20 +164,28 @@ def tile_pairconnect_s_kernel(tc, x, W1, b1, W2, b2, out):
         regroup_w1(nc.scalar.copy, 1, scalar_cols)
         quantise_w1(0)
         quantise_w1(1)
-        quantise_x(0, RUN_AT)
-        quantise_x(RUN_AT + POSITIONS, len(BLOCK_ORDER) - RUN_AT - POSITIONS)
-        b1_f32 = keep.tile([P, PACK], F32)
-        nc.vector.tensor_copy(out=b1_f32[:], in_=b1_bf[:])
+        def extras():
+            for block in range(len(BLOCK_ORDER)):
+                if not RUN_AT <= block < RUN_AT + POSITIONS:
+                    for g in range(2):
+                        nc.scalar.copy(
+                            out=x_grouped_words[:, g, block], in_=x_t_by_position[g][:, BLOCK_ORDER[block]]
+                        )
+        b2_all = keep.tile([P, O], F32)
+
+        def b2_copy():
+            nc.scalar.copy(out=b2_all[:], in_=b2_ps[:])
 
         w2_grouped = keep.tile([P, O, PACK], BF16, align_bytes=64)
-        nc.scalar.copy(
-            out=w2_grouped[:].rearrange("p (c i) j -> p c j i", i=4),
-            in_=w2_rows[:].rearrange("p j (c i) -> p c j i", i=4),
-        )
-        b2_all = keep.tile([P, O], F32)
         w2_codes = keep.tile([P, O], U32, align_bytes=64)
         w2_scales = keep.tile([P, O], U8, align_bytes=64)
         w2_parts = ((0, 256), (256, 384))
+
+        def regroup_w2(copy):
+            copy(
+                out=w2_grouped[:].rearrange("p (c i) j -> p c j i", i=4),
+                in_=w2_rows[:].rearrange("p j (c i) -> p c j i", i=4),
+            )
 
         def quantise_w2():
             flat = w2_grouped[:].rearrange("p o j -> p (o j)")
@@ -189,51 +196,70 @@ def tile_pairconnect_s_kernel(tc, x, W1, b1, W2, b2, out):
                     in_=flat[:, lo * PACK : hi * PACK],
                 )
 
+        h_chunks = keep.tile([P, TILES, PACK, P], BF16)
+        h_grouped = keep.tile([P, TILES, P * PACK], BF16, align_bytes=64)
         h_codes = keep.tile([P, TILES, P], U32, align_bytes=64)
         h_scales = keep.tile([P, TILES, P], U8, align_bytes=64)
         p_all = keep.tile([P, TILES, O], F32)
         p_squared = keep.tile([P, TILES, O], F32)
         quarter_norm2 = keep.tile([P, TILES], F32)
+        half_norm = keep.tile([P, TILES - 1], F32)
         pre_tiles = {}
-        h_tiles = {}
         q_tiles = {}
 
-        def stage1(m):
+        def x_start(m, half):
             (i_low, j_low), (i_high, j_high) = PAIRS[m]
-            pre = psum_pre.tile([P, PACK, P], F32, name="pre")
-            pre_tiles[m] = pre
-            starts = (first_block(i_low, i_high) * HALF, first_block(j_low, j_high) * HALF)
+            low, high = ((i_low, i_high), (j_low, j_high))[half]
+            return first_block(low, high) * HALF
+
+        def stage1_pass(m, t, half):
+            w_cols = slice((half * PACK + t) * P, (half * PACK + t + 1) * P)
+            x_cols = slice(x_start(m, half), x_start(m, half) + P)
+            nc.tensor.matmul_mx(
+                out=pre_tiles[m, t],
+                lhsT=w1_codes[:, w_cols].bitcast(FP8X4),
+                lhsT_scale=w1_scales[:, w_cols],
+                rhs=x_codes[:, x_cols].bitcast(FP8X4),
+                rhs_scale=x_scales[:, x_cols],
+                start=(half == 0),
+                stop=(half == 1),
+            )
+
+        def stage1_spread():
             for t in range(PACK):
+                pre = banks.tile([P, P], F32, name="bank%d" % (3 + t))
+                pre_tiles[0, t] = pre[:]
+            for half in range(2):
+                for t in range(PACK):
+                    stage1_pass(0, t, half)
+
+        def stage1(m, bank):
+            pre = banks.tile([P, PACK, P], F32, name="bank%d" % bank)
+            for t in range(PACK):
+                pre_tiles[m, t] = pre[:, t, :]
                 for half in range(2):
-                    w_cols = slice((half * PACK + t) * P, (half * PACK + t + 1) * P)
-                    x_cols = slice(starts[half], starts[half] + P)
-                    nc.tensor.matmul_mx(
-                        out=pre[:, t, :],
-                        lhsT=w1_codes[:, w_cols].bitcast(FP8X4),
-                        lhsT_scale=w1_scales[:, w_cols],
-                        rhs=x_codes[:, x_cols].bitcast(FP8X4),
-                        rhs_scale=x_scales[:, x_cols],
-                        start=(half == 0),
-                        stop=(half == 1),
-                    )
+                    stage1_pass(m, t, half)
 
         def add_b1_and_gelu(m):
-            v = work.tile([P, P, PACK], F32, name="v")
-            nc.vector.tensor_tensor(
-                out=v[:],
-                in0=pre_tiles[m][:].rearrange("q t w -> q w t"),
-                in1=b1_f32[:].unsqueeze(1).to_broadcast([P, P, PACK]),
-                op=ALU.add,
+            for t in range(PACK):
+                nc.scalar.activation(
+                    out=h_chunks[:, m, t, :],
+                    in_=pre_tiles[m, t],
+                    func=ACT.Gelu,
+                    bias=b1_bf[:, t : t + 1],
+                )
+
+        def group_h(m):
+            nc.vector.tensor_copy(
+                out=h_grouped[:, m].rearrange("q (c i t) -> q c t i", i=4, t=PACK),
+                in_=h_chunks[:, m].rearrange("q t (c i) -> q c t i", i=4),
             )
-            h = work.tile([P, P * PACK], BF16, name="h", align_bytes=64)
-            h_tiles[m] = h
-            nc.scalar.activation(out=h[:], in_=v[:].rearrange("q w t -> q (w t)"), func=ACT.Gelu)
 
         def quantise_h_and_stage2(m):
             nc.vector.quantize_mx(
-                out=h_codes[:, m, :].bitcast(FP8X4), scales=h_scales[:, m, :], in_=h_tiles[m][:]
+                out=h_codes[:, m, :].bitcast(FP8X4), scales=h_scales[:, m, :], in_=h_grouped[:, m]
             )
-            q = psum_q.tile([P, O], F32, name="q")
+            q = banks.tile([P, O], F32, name="bank%d" % Q_BANKS[m])
             q_tiles[m] = q
             for lo, hi in w2_parts:
                 nc.tensor.matmul_mx(
@@ -246,10 +272,12 @@ def tile_pairconnect_s_kernel(tc, x, W1, b1, W2, b2, out):
                     stop=True,
                 )
 
-        def add_b2_and_norm(m):
+        def add_b2(m):
             nc.vector.tensor_tensor(
                 out=p_all[:, m, :], in0=q_tiles[m][:], in1=b2_all[:], op=ALU.add
             )
+
+        def square(m):
             nc.scalar.activation(
                 out=p_squared[:, m, :],
                 in_=p_all[:, m, :],
@@ -257,111 +285,143 @@ def tile_pairconnect_s_kernel(tc, x, W1, b1, W2, b2, out):
                 scale=0.5,
                 accum_out=quarter_norm2[:, m : m + 1],
             )
-            for a in range(2):
-                sides = [side for side in range(2) if result_of(m, side) == a]
-                if sides:
-                    rows = slice(sides[0] * HALF, (sides[-1] + 1) * HALF)
-                    nc.gpsimd.tensor_tensor(
-                        out=half_norm[rows, a, m : m + 1],
-                        in0=quarter_norm2[rows, m : m + 1],
-                        in1=half_power[rows, :],
-                        op=ALU.pow,
-                    )
 
-        for m in range(PRE_AHEAD):
-            stage1(m)
-        for step in range(TILES + 2):
-            if step + PRE_AHEAD < TILES:
-                stage1(step + PRE_AHEAD)
-            if step < TILES:
-                add_b1_and_gelu(step)
-            if step == 0:
-                quantise_w2()
-                nc.scalar.copy(out=b2_all[:], in_=b2_ps[:])
-            if 1 <= step <= TILES:
-                quantise_h_and_stage2(step - 1)
-            if step >= 2:
-                add_b2_and_norm(step - 2)
+        def root(out, lo, hi, rows):
+            nc.gpsimd.tensor_tensor(
+                out=out,
+                in0=quarter_norm2[rows, lo:hi],
+                in1=half_power[rows, 0 : hi - lo],
+                op=ALU.pow,
+            )
 
+        low, high, both = slice(0, HALF), slice(HALF, P), slice(0, P)
+
+        extras()
+        b2_copy()
+        regroup_w2(nc.vector.tensor_copy)
+        quantise_x(0, RUN_AT)
+        quantise_x(RUN_AT + POSITIONS, len(BLOCK_ORDER) - RUN_AT - POSITIONS)
+        quantise_w2()
+        stage1_spread()
+        add_b1_and_gelu(0)
+        stage1(1, 7)
+        add_b1_and_gelu(1)
+        group_h(0)
+        stage1(2, 0)
+        add_b1_and_gelu(2)
+        stage1(3, 1)
+        quantise_h_and_stage2(0)
+        add_b1_and_gelu(3)
+        stage1(4, 3)
+        group_h(1)
+        quantise_h_and_stage2(1)
+        add_b1_and_gelu(4)
+        for m in range(2, TILES):
+            group_h(m)
+            add_b2(m - 2)
+            square(m - 2)
+            quantise_h_and_stage2(m)
+        root(half_norm[:, 0:1], 0, 1, both)
         out_by_row = out.rearrange("b i o -> i b o")
 
-        def store(a, result):
+        def store(a, result, queue):
             for side in range(2):
                 rows = slice(side * HALF, (side + 1) * HALF)
-                nc.sync.dma_start(out=out_by_row[ROWS_OF_RESULT[a][side]], in_=result[rows, :])
+                queue.dma_start(out=out_by_row[ROWS_OF_RESULT[a][side]], in_=result[rows, :])
 
-        first, last = tiles_of_result(SHORT)[0], tiles_of_result(SHORT)[1] - 1
-        assert last == first + 1
-        difference = keep.tile([P, O], F32)
-        nc.vector.tensor_tensor(
-            out=difference[:], in0=p_all[:, last, :], in1=p_all[:, first, :], op=ALU.subtract
-        )
+        def column(name):
+            return keep.tile([P, 1], F32, name=name)
 
-        lo, hi = tiles_of_result(LONG)
-        neg_largest = keep.tile([P, 1], F32)
-        nc.vector.tensor_reduce(
-            out=neg_largest[:], in_=half_norm[:, LONG, lo:hi], axis=AXIS.X, op=ALU.max, negate=True
-        )
-        tanh = keep.tile([P, hi - lo], F32)
-        nc.scalar.activation(
-            out=tanh[:], in_=half_norm[:, LONG, lo:hi], func=ACT.Tanh, bias=neg_largest[:]
-        )
-        tanh_short = keep.tile([P, 1], F32)
-        nc.scalar.activation(
-            out=tanh_short[:],
-            in_=half_norm[:, SHORT, first : first + 1],
-            func=ACT.Tanh,
-            scale=-1.0,
-            bias=half_norm[:, SHORT, last : last + 1],
-        )
-        denominator = keep.tile([P, hi - lo], F32)
-        nc.vector.tensor_scalar(
-            out=denominator[:], in0=tanh[:], scalar1=-1.0, scalar2=1.0, op0=ALU.mult, op1=ALU.add
-        )
-        nc.vector.reciprocal(out=denominator[:], in_=denominator[:])
-        expd = keep.tile([P, hi - lo], F32)
-        total = keep.tile([P, 1], F32)
-        nc.vector.scalar_tensor_tensor(
-            out=expd[:],
-            in0=tanh[:],
-            scalar=1.0,
-            in1=denominator[:],
-            op0=ALU.add,
-            op1=ALU.mult,
-            accum_out=total[:],
-        )
-        inverse = keep.tile([P, 1], F32)
-        nc.vector.reciprocal(out=inverse[:], in_=total[:])
-        weight = keep.tile([P, hi - lo], F32)
-        nc.vector.tensor_scalar(
-            out=weight[:], in0=expd[:], scalar1=inverse[:], scalar2=None, op0=ALU.mult
-        )
+        def wide(name):
+            return keep.tile([P, O], F32, name=name)
 
-        long_result = keep.tile([P, O], F32)
-        nc.scalar.activation(
-            out=long_result[:], in_=p_all[:, lo, :], func=ACT.Copy, scale=weight[:, 0:1]
-        )
-        weight_last = keep.tile([P, 1], F32)
-        nc.vector.tensor_scalar(
-            out=weight_last[:], in0=tanh_short[:], scalar1=0.5, scalar2=0.5, op0=ALU.mult, op1=ALU.add
-        )
-        short_result = keep.tile([P, O], F32)
-        nc.vector.scalar_tensor_tensor(
-            out=short_result[:],
-            in0=difference[:],
-            scalar=weight_last[:],
-            in1=p_all[:, first, :],
-            op0=ALU.mult,
-            op1=ALU.add,
-        )
-        store(SHORT, short_result)
-        for m in range(lo + 1, hi):
+        def tanh(name, n, bias, scale=1.0):
+            t = column(name)
+            nc.scalar.activation(out=t[:], in_=half_norm[:, n : n + 1], func=ACT.Tanh, bias=bias, scale=scale)
+            return t
+
+        def minus(name, a, b):
+            d = wide(name)
+            nc.vector.tensor_tensor(out=d[:], in0=a, in1=b, op=ALU.subtract)
+            return d
+
+        def merge(name, base, difference, weight):
+            r = wide(name)
             nc.vector.scalar_tensor_tensor(
-                out=long_result[:],
-                in0=p_all[:, m, :],
-                scalar=weight[:, m - lo : m - lo + 1],
-                in1=long_result[:],
-                op0=ALU.mult,
-                op1=ALU.add,
+                out=r[:], in0=difference[:], scalar=weight[:], in1=base, op0=ALU.mult, op1=ALU.add
             )
-        store(LONG, long_result)
+            return r
+
+        def affine(name, t, mult, add):
+            a = column(name)
+            nc.vector.tensor_scalar(out=a[:], in0=t[:], scalar1=mult, scalar2=add, op0=ALU.mult, op1=ALU.add)
+            return a
+
+        def magnitude(name, t):
+            a = column(name)
+            nc.vector.scalar_tensor_tensor(out=a[:], in0=t[:], scalar=-1.0, in1=t[:], op0=ALU.mult, op1=ALU.max)
+            return a
+
+        def plus_one_times(name, t, factor):
+            a = column(name)
+            nc.vector.scalar_tensor_tensor(out=a[:], in0=t[:], scalar=1.0, in1=factor[:], op0=ALU.add, op1=ALU.mult)
+            return a
+
+        def reciprocal(name, t):
+            a = column(name)
+            nc.vector.reciprocal(out=a[:], in_=t[:])
+            return a
+
+        def negmax(out, rows, n):
+            nc.vector.tensor_reduce(out=out, in_=half_norm[rows, 0:n], axis=AXIS.X, op=ALU.max, negate=True)
+
+        def p_of(m):
+            return p_all[:, m, :]
+
+        neg_max1 = column("neg_max1")
+        add_b2(3)
+        root(half_norm[:, 1:2], 1, 2, both)
+        t1 = tanh("t1", 0, half_norm[:, 1:2], -1.0)
+        square(3)
+        root(half_norm[:, 2:3], 2, 3, both)
+        d1 = minus("d1", p_of(1), p_of(0))
+        add_b2(4)
+        negmax(neg_max1[:], both, 2)
+        t2 = tanh("t2", 2, neg_max1[:])
+        square(4)
+        root(half_norm[:, 3:4], 3, 4, both)
+        root(short_bias[low, :], 4, 5, low)
+        w1 = affine("w1", t1, 0.5, 0.5)
+        a1 = magnitude("a1", t1)
+        r1 = merge("r1", p_of(0), d1, w1)
+        am = affine("am", a1, 1.0, -1.0)
+        ap = affine("ap", a1, 1.0, 3.0)
+        aa = affine("aa", a1, 1.0, 1.0)
+        negmax(long_bias[high, :], high, 3)
+        t3 = tanh("t3", 3, long_bias[:])
+        tS = tanh("tS", 3, short_bias[:], -1.0)
+        den2 = affine("den2", t2, am[:], ap[:])
+        num2 = plus_one_times("num2", t2, aa)
+        d2 = minus("d2", p_of(2), r1[:])
+        rden2 = reciprocal("rden2", den2)
+        abs2 = magnitude("abs2", t2)
+        w2 = column("w2")
+        nc.vector.tensor_tensor(out=w2[:], in0=num2[:], in1=rden2[:], op=ALU.mult)
+        a2 = plus_one_times("a2", abs2, aa)
+        r2 = merge("r2", r1[:], d2, w2)
+        am2 = column("am2")
+        nc.vector.tensor_tensor(out=am2[:], in0=a2[:], in1=den2[:], op=ALU.subtract)
+        ap2 = column("ap2")
+        nc.vector.tensor_tensor(out=ap2[:], in0=a2[:], in1=den2[:], op=ALU.add)
+        dS = minus("dS", p_of(4), p_of(3))
+        den3 = affine("den3", t3, am2[:], ap2[:])
+        num3 = plus_one_times("num3", t3, a2)
+        wS = affine("wS", tS, 0.5, 0.5)
+        rden3 = reciprocal("rden3", den3)
+        d3 = minus("d3", p_of(3), r2[:])
+        w3 = column("w3")
+        nc.vector.tensor_tensor(out=w3[:], in0=num3[:], in1=rden3[:], op=ALU.mult)
+        rS = merge("rS", p_of(3), dS, wS)
+        store(SHORT, rS, nc.scalar)
+        r3 = merge("r3", r2[:], d3, w3)
+        store(LONG, r3, nc.sync)

@@ -84,18 +84,25 @@ def tile_pairconnect_s_kernel(tc, x, W1, b1, W2, b2, out):
             )
         w2_rows = keep.tile([P, PACK, O], BF16)
         nc.sync.dma_start(out=w2_rows[:], in_=W2.rearrange("(p j) o -> p j o", j=PACK))
+        ones = keep.tile([P, P], BF16)
+        nc.vector.memset(ones[:], 1.0)
 
         zero = keep.tile([P, 1], F32)
         nc.vector.memset(zero[:], 0.0)
         warm = keep.tile([P, 1], F32)
         nc.scalar.activation(out=warm[:], in_=zero[:], func=ACT.Gelu)
 
-        ones = keep.tile([P, P], BF16)
-        nc.vector.memset(ones[:], 1.0)
         ident = keep.tile([P, P], F32)
         masks.make_identity(nc, ident[:])
         half_power = keep.tile([P, TILES], F32)
         nc.gpsimd.memset(half_power[:], 0.5)
+        def constant(name, value):
+            c = keep.tile([P, 1], F32, name=name)
+            nc.gpsimd.memset(c[:], value)
+            return c[:]
+
+        half = half_power[:, 0:1]
+        plus_one, minus_one, plus_three = constant("c1", 1.0), constant("cm1", -1.0), constant("c3", 3.0)
         long_bias = keep.tile([P, 1], F32)
         nc.gpsimd.memset(long_bias[:], NEG)
         short_bias = keep.tile([P, 1], F32)
@@ -127,8 +134,13 @@ def tile_pairconnect_s_kernel(tc, x, W1, b1, W2, b2, out):
                 in_=x_grouped[:, first * HALF * PACK : (first + blocks) * HALF * PACK],
             )
 
+
         b2_ps = banks.tile([P, O], F32, name="bank2")
         nc.tensor.matmul(out=b2_ps[:], lhsT=ones[:], rhs=b2_row[:], start=True, stop=True)
+        b2_all = keep.tile([P, O], F32)
+
+        def b2_copy():
+            nc.scalar.copy(out=b2_all[:], in_=b2_ps[:])
 
         w1_grouped = keep.tile([P, 2 * PACK * F], BF16, align_bytes=64)
         w1_grouped_view = w1_grouped[:].rearrange(
@@ -155,8 +167,8 @@ def tile_pairconnect_s_kernel(tc, x, W1, b1, W2, b2, out):
         vector_cols = slice(0, W1_VECTOR_COLS)
         scalar_cols = slice(W1_VECTOR_COLS, P)
         run = slice(RUN_AT, RUN_AT + POSITIONS)
-        nc.vector.tensor_copy(out=x_grouped_words[:, 0, run], in_=x_t_by_position[0])
-        nc.scalar.copy(out=x_grouped_words[:, 1, run], in_=x_t_by_position[1])
+        for g in range(2):
+            nc.scalar.copy(out=x_grouped_words[:, g, run], in_=x_t_by_position[g])
         regroup_w1(nc.vector.tensor_copy, 0, vector_cols)
         regroup_w1(nc.scalar.copy, 0, scalar_cols)
         quantise_x(RUN_AT, POSITIONS)
@@ -171,25 +183,21 @@ def tile_pairconnect_s_kernel(tc, x, W1, b1, W2, b2, out):
                         nc.scalar.copy(
                             out=x_grouped_words[:, g, block], in_=x_t_by_position[g][:, BLOCK_ORDER[block]]
                         )
-        b2_all = keep.tile([P, O], F32)
-
-        def b2_copy():
-            nc.scalar.copy(out=b2_all[:], in_=b2_ps[:])
 
         w2_grouped = keep.tile([P, O, PACK], BF16, align_bytes=64)
         w2_codes = keep.tile([P, O], U32, align_bytes=64)
         w2_scales = keep.tile([P, O], U8, align_bytes=64)
         w2_parts = ((0, 256), (256, 384))
 
-        def regroup_w2(copy):
+        def regroup_w2(copy, lo, hi):
             copy(
-                out=w2_grouped[:].rearrange("p (c i) j -> p c j i", i=4),
-                in_=w2_rows[:].rearrange("p j (c i) -> p c j i", i=4),
+                out=w2_grouped[:, lo:hi].rearrange("p (c i) j -> p c j i", i=4),
+                in_=w2_rows[:, :, lo:hi].rearrange("p j (c i) -> p c j i", i=4),
             )
 
-        def quantise_w2():
+        def quantise_w2(part):
             flat = w2_grouped[:].rearrange("p o j -> p (o j)")
-            for lo, hi in w2_parts:
+            for lo, hi in w2_parts[part:part+1]:
                 nc.vector.quantize_mx(
                     out=w2_codes[:, lo:hi].bitcast(FP8X4),
                     scales=w2_scales[:, lo:hi],
@@ -296,16 +304,18 @@ def tile_pairconnect_s_kernel(tc, x, W1, b1, W2, b2, out):
 
         low, high, both = slice(0, HALF), slice(HALF, P), slice(0, P)
 
+        regroup_w2(nc.vector.tensor_copy, 0, 256)
+        regroup_w2(nc.scalar.copy, 256, 384)
         extras()
-        b2_copy()
-        regroup_w2(nc.vector.tensor_copy)
         quantise_x(0, RUN_AT)
         quantise_x(RUN_AT + POSITIONS, len(BLOCK_ORDER) - RUN_AT - POSITIONS)
-        quantise_w2()
+        quantise_w2(0)
         stage1_spread()
         add_b1_and_gelu(0)
+        b2_copy()
         stage1(1, 7)
         add_b1_and_gelu(1)
+        quantise_w2(1)
         group_h(0)
         stage1(2, 0)
         add_b1_and_gelu(2)
@@ -340,17 +350,15 @@ def tile_pairconnect_s_kernel(tc, x, W1, b1, W2, b2, out):
             nc.scalar.activation(out=t[:], in_=half_norm[:, n : n + 1], func=ACT.Tanh, bias=bias, scale=scale)
             return t
 
-        def minus(name, a, b):
-            d = wide(name)
-            nc.vector.tensor_tensor(out=d[:], in0=a, in1=b, op=ALU.subtract)
-            return d
+        CUTS = (slice(0, O // 2), slice(O // 2, O))
 
-        def merge(name, base, difference, weight):
-            r = wide(name)
+        def minus(out, a, b):
+            nc.vector.tensor_tensor(out=out, in0=a, in1=b, op=ALU.subtract)
+
+        def weigh(out, part, weight, rest):
             nc.vector.scalar_tensor_tensor(
-                out=r[:], in0=difference[:], scalar=weight[:], in1=base, op0=ALU.mult, op1=ALU.add
+                out=out, in0=part, scalar=weight[:], in1=rest, op0=ALU.mult, op1=ALU.add
             )
-            return r
 
         def affine(name, t, mult, add):
             a = column(name)
@@ -367,6 +375,11 @@ def tile_pairconnect_s_kernel(tc, x, W1, b1, W2, b2, out):
             nc.vector.scalar_tensor_tensor(out=a[:], in0=t[:], scalar=1.0, in1=factor[:], op0=ALU.add, op1=ALU.mult)
             return a
 
+        def line(name, t, scale, bias):
+            a = column(name)
+            nc.scalar.activation(out=a[:], in_=t[:], func=ACT.Identity, scale=scale, bias=bias)
+            return a
+
         def reciprocal(name, t):
             a = column(name)
             nc.vector.reciprocal(out=a[:], in_=t[:])
@@ -375,53 +388,65 @@ def tile_pairconnect_s_kernel(tc, x, W1, b1, W2, b2, out):
         def negmax(out, rows, n):
             nc.vector.tensor_reduce(out=out, in_=half_norm[rows, 0:n], axis=AXIS.X, op=ALU.max, negate=True)
 
-        def p_of(m):
-            return p_all[:, m, :]
+        def p_of(m, cut=slice(0, O)):
+            return p_all[:, m, cut]
+
+        def pair(name, a, b, op):
+            r = column(name)
+            nc.vector.tensor_tensor(out=r[:], in0=a[:], in1=b[:], op=op)
+            return r
 
         neg_max1 = column("neg_max1")
+        d1, r1, d2, r2, d3, r3, uS, rS = [wide(n) for n in ("d1", "r1", "d2", "r2", "d3", "r3", "uS", "rS")]
+        A, B = CUTS
         add_b2(3)
         root(half_norm[:, 1:2], 1, 2, both)
         t1 = tanh("t1", 0, half_norm[:, 1:2], -1.0)
         square(3)
         root(half_norm[:, 2:3], 2, 3, both)
-        d1 = minus("d1", p_of(1), p_of(0))
-        add_b2(4)
+        minus(d1[:], p_of(1), p_of(0))
         negmax(neg_max1[:], both, 2)
+        w1 = affine("w1", t1, 0.5, 0.5)
+        add_b2(4)
+        a1 = column("a1")
+        nc.scalar.activation(out=a1[:], in_=t1[:], func=ACT.Abs)
+        aa = line("aa", a1, 1.0, plus_one)
+        am = line("am", a1, 1.0, minus_one)
+        ap = line("ap", a1, 1.0, plus_three)
         t2 = tanh("t2", 2, neg_max1[:])
         square(4)
         root(half_norm[:, 3:4], 3, 4, both)
         root(short_bias[low, :], 4, 5, low)
-        w1 = affine("w1", t1, 0.5, 0.5)
-        a1 = magnitude("a1", t1)
-        r1 = merge("r1", p_of(0), d1, w1)
-        am = affine("am", a1, 1.0, -1.0)
-        ap = affine("ap", a1, 1.0, 3.0)
-        aa = affine("aa", a1, 1.0, 1.0)
+        for cut in CUTS:
+            weigh(r1[:, cut], d1[:, cut], w1, p_of(0, cut))
         negmax(long_bias[high, :], high, 3)
         t3 = tanh("t3", 3, long_bias[:])
         tS = tanh("tS", 3, short_bias[:], -1.0)
+        vS = line("vS", tS, -0.5, half)
+        wS = line("wS", tS, 0.5, half)
         den2 = affine("den2", t2, am[:], ap[:])
         num2 = plus_one_times("num2", t2, aa)
-        d2 = minus("d2", p_of(2), r1[:])
-        rden2 = reciprocal("rden2", den2)
         abs2 = magnitude("abs2", t2)
-        w2 = column("w2")
-        nc.vector.tensor_tensor(out=w2[:], in0=num2[:], in1=rden2[:], op=ALU.mult)
+        minus(d2[:, A], p_of(2, A), r1[:, A])
+        rden2 = reciprocal("rden2", den2)
         a2 = plus_one_times("a2", abs2, aa)
-        r2 = merge("r2", r1[:], d2, w2)
-        am2 = column("am2")
-        nc.vector.tensor_tensor(out=am2[:], in0=a2[:], in1=den2[:], op=ALU.subtract)
-        ap2 = column("ap2")
-        nc.vector.tensor_tensor(out=ap2[:], in0=a2[:], in1=den2[:], op=ALU.add)
-        dS = minus("dS", p_of(4), p_of(3))
-        den3 = affine("den3", t3, am2[:], ap2[:])
+        minus(d2[:, B], p_of(2, B), r1[:, B])
+        w2 = pair("w2", num2, rden2, ALU.mult)
+        am2 = pair("am2", a2, den2, ALU.subtract)
+        ap2 = pair("ap2", a2, den2, ALU.add)
         num3 = plus_one_times("num3", t3, a2)
-        wS = affine("wS", tS, 0.5, 0.5)
+        den3 = affine("den3", t3, am2[:], ap2[:])
+        weigh(r2[:, A], d2[:, A], w2, r1[:, A])
         rden3 = reciprocal("rden3", den3)
-        d3 = minus("d3", p_of(3), r2[:])
-        w3 = column("w3")
-        nc.vector.tensor_tensor(out=w3[:], in0=num3[:], in1=rden3[:], op=ALU.mult)
-        rS = merge("rS", p_of(3), dS, wS)
-        store(SHORT, rS, nc.scalar)
-        r3 = merge("r3", r2[:], d3, w3)
+        weigh(r2[:, B], d2[:, B], w2, r1[:, B])
+        w3 = pair("w3", num3, rden3, ALU.mult)
+        for cut in CUTS:
+            minus(d3[:, cut], p_of(3, cut), r2[:, cut])
+        for cut in CUTS:
+            nc.scalar.activation(out=uS[:, cut], in_=p_of(3, cut), func=ACT.Copy, scale=vS[:])
+        for cut in CUTS:
+            weigh(r3[:, cut], d3[:, cut], w3, r2[:, cut])
         store(LONG, r3, nc.sync)
+        for cut in CUTS:
+            weigh(rS[:, cut], p_of(4, cut), wS, uS[:, cut])
+        store(SHORT, rS, nc.scalar)

@@ -6,6 +6,7 @@ import concourse.mybir as mybir
 F32 = mybir.dt.float32
 BF16 = mybir.dt.bfloat16
 U32 = mybir.dt.uint32
+I32 = mybir.dt.int32
 U8 = mybir.dt.uint8
 FP8X4 = mybir.dt.float8_e4m3fn_x4
 ACT = mybir.ActivationFunctionType
@@ -24,8 +25,8 @@ PAIRS = (
     ((2, 0), (3, 1)),
     ((2, 1), (3, 2)),
     ((2, 2), (3, 3)),
-    ((1, 0), (3, 0)),
-    ((1, 1), (0, 0)),
+    ((1, 1), (3, 0)),
+    ((1, 0), (0, 0)),
 )
 TILES = len(PAIRS)
 ROWS_OF_RESULT = ((2, 3), (1, 0))
@@ -103,10 +104,6 @@ def tile_pairconnect_s_kernel(tc, x, W1, b1, W2, b2, out):
 
         half = half_power[:, 0:1]
         plus_one, minus_one, plus_three = constant("c1", 1.0), constant("cm1", -1.0), constant("c3", 3.0)
-        long_bias = keep.tile([P, 1], F32)
-        nc.gpsimd.memset(long_bias[:], NEG)
-        short_bias = keep.tile([P, 1], F32)
-        nc.gpsimd.memset(short_bias[:], -NEG)
 
         x_words = x_rows[:].bitcast(F32).rearrange("r (g p u) -> r g u p", g=2, u=2)
         x_t = []
@@ -176,13 +173,13 @@ def tile_pairconnect_s_kernel(tc, x, W1, b1, W2, b2, out):
         regroup_w1(nc.scalar.copy, 1, scalar_cols)
         quantise_w1(0)
         quantise_w1(1)
-        def extras():
+        def duplicate_blocks():
             for block in range(len(BLOCK_ORDER)):
                 if not RUN_AT <= block < RUN_AT + POSITIONS:
-                    for g in range(2):
-                        nc.scalar.copy(
-                            out=x_grouped_words[:, g, block], in_=x_t_by_position[g][:, BLOCK_ORDER[block]]
-                        )
+                    src = slice((RUN_AT + BLOCK_ORDER[block]) * HALF, (RUN_AT + BLOCK_ORDER[block] + 1) * HALF)
+                    dst = slice(block * HALF, (block + 1) * HALF)
+                    nc.sync.dma_start(out=x_codes[:, dst].bitcast(I32), in_=x_codes[:, src].bitcast(I32))
+                    nc.sync.dma_start(out=x_scales[:, dst], in_=x_scales[:, src])
 
         w2_grouped = keep.tile([P, O, PACK], BF16, align_bytes=64)
         w2_codes = keep.tile([P, O], U32, align_bytes=64)
@@ -211,7 +208,7 @@ def tile_pairconnect_s_kernel(tc, x, W1, b1, W2, b2, out):
         p_all = keep.tile([P, TILES, O], F32)
         p_squared = keep.tile([P, TILES, O], F32)
         quarter_norm2 = keep.tile([P, TILES], F32)
-        half_norm = keep.tile([P, TILES - 1], F32)
+        half_norm = keep.tile([P, TILES], F32)
         pre_tiles = {}
         q_tiles = {}
 
@@ -257,8 +254,8 @@ def tile_pairconnect_s_kernel(tc, x, W1, b1, W2, b2, out):
                     bias=b1_bf[:, t : t + 1],
                 )
 
-        def group_h(m):
-            nc.vector.tensor_copy(
+        def group_h(m, copy=nc.vector.tensor_copy):
+            copy(
                 out=h_grouped[:, m].rearrange("q (c i t) -> q c t i", i=4, t=PACK),
                 in_=h_chunks[:, m].rearrange("q t (c i) -> q c t i", i=4),
             )
@@ -306,9 +303,7 @@ def tile_pairconnect_s_kernel(tc, x, W1, b1, W2, b2, out):
 
         regroup_w2(nc.vector.tensor_copy, 0, 256)
         regroup_w2(nc.scalar.copy, 256, 384)
-        extras()
-        quantise_x(0, RUN_AT)
-        quantise_x(RUN_AT + POSITIONS, len(BLOCK_ORDER) - RUN_AT - POSITIONS)
+        duplicate_blocks()
         quantise_w2(0)
         stage1_spread()
         add_b1_and_gelu(0)
@@ -326,18 +321,25 @@ def tile_pairconnect_s_kernel(tc, x, W1, b1, W2, b2, out):
         group_h(1)
         quantise_h_and_stage2(1)
         add_b1_and_gelu(4)
-        for m in range(2, TILES):
-            group_h(m)
-            add_b2(m - 2)
-            square(m - 2)
-            quantise_h_and_stage2(m)
+        group_h(2)
+        add_b2(0)
+        square(0)
+        quantise_h_and_stage2(2)
+
+        group_h(3)
+        add_b2(1)
+        square(1)
+
+        quantise_h_and_stage2(3)
+        group_h(4)
+        add_b2(2)
+        square(2)
+        quantise_h_and_stage2(4)
         root(half_norm[:, 0:1], 0, 1, both)
         out_by_row = out.rearrange("b i o -> i b o")
 
-        def store(a, result, queue):
-            for side in range(2):
-                rows = slice(side * HALF, (side + 1) * HALF)
-                queue.dma_start(out=out_by_row[ROWS_OF_RESULT[a][side]], in_=result[rows, :])
+        def store(queue, i, rows, result):
+            queue.dma_start(out=out_by_row[i], in_=result[rows, :])
 
         def column(name):
             return keep.tile([P, 1], F32, name=name)
@@ -345,24 +347,23 @@ def tile_pairconnect_s_kernel(tc, x, W1, b1, W2, b2, out):
         def wide(name):
             return keep.tile([P, O], F32, name=name)
 
-        def tanh(name, n, bias, scale=1.0):
-            t = column(name)
-            nc.scalar.activation(out=t[:], in_=half_norm[:, n : n + 1], func=ACT.Tanh, bias=bias, scale=scale)
-            return t
-
         CUTS = (slice(0, O // 2), slice(O // 2, O))
+        A, B = CUTS
+
+        def tanh(name, rows, n, bias, scale=1.0):
+            t = column(name)
+            nc.scalar.activation(out=t[rows, :], in_=half_norm[rows, n : n + 1], func=ACT.Tanh, bias=bias, scale=scale)
+            return t
 
         def minus(out, a, b):
             nc.vector.tensor_tensor(out=out, in0=a, in1=b, op=ALU.subtract)
 
         def weigh(out, part, weight, rest):
-            nc.vector.scalar_tensor_tensor(
-                out=out, in0=part, scalar=weight[:], in1=rest, op0=ALU.mult, op1=ALU.add
-            )
+            nc.vector.scalar_tensor_tensor(out=out, in0=part, scalar=weight[:], in1=rest, op0=ALU.mult, op1=ALU.add)
 
-        def affine(name, t, mult, add):
+        def affine(name, rows, t, mult, add):
             a = column(name)
-            nc.vector.tensor_scalar(out=a[:], in0=t[:], scalar1=mult, scalar2=add, op0=ALU.mult, op1=ALU.add)
+            nc.vector.tensor_scalar(out=a[rows, :], in0=t[rows, :], scalar1=mult, scalar2=add, op0=ALU.mult, op1=ALU.add)
             return a
 
         def magnitude(name, t):
@@ -370,83 +371,85 @@ def tile_pairconnect_s_kernel(tc, x, W1, b1, W2, b2, out):
             nc.vector.scalar_tensor_tensor(out=a[:], in0=t[:], scalar=-1.0, in1=t[:], op0=ALU.mult, op1=ALU.max)
             return a
 
-        def plus_one_times(name, t, factor):
+        def plus_one_times(name, rows, t, factor):
             a = column(name)
-            nc.vector.scalar_tensor_tensor(out=a[:], in0=t[:], scalar=1.0, in1=factor[:], op0=ALU.add, op1=ALU.mult)
+            nc.vector.scalar_tensor_tensor(out=a[rows, :], in0=t[rows, :], scalar=1.0, in1=factor[rows, :], op0=ALU.add, op1=ALU.mult)
             return a
 
-        def line(name, t, scale, bias):
+        def reciprocal(name, rows, t):
             a = column(name)
-            nc.scalar.activation(out=a[:], in_=t[:], func=ACT.Identity, scale=scale, bias=bias)
+            nc.vector.reciprocal(out=a[rows, :], in_=t[rows, :])
             return a
 
-        def reciprocal(name, t):
-            a = column(name)
-            nc.vector.reciprocal(out=a[:], in_=t[:])
-            return a
+        def line(out, rows, t, scale, bias):
+            nc.scalar.activation(out=out[rows, :], in_=t[rows, :], func=ACT.Identity, scale=scale, bias=bias[rows, :])
+            return out
 
-        def negmax(out, rows, n):
-            nc.vector.tensor_reduce(out=out, in_=half_norm[rows, 0:n], axis=AXIS.X, op=ALU.max, negate=True)
+        def negmax(name, rows, n):
+            a = column(name)
+            nc.vector.tensor_reduce(out=a[rows, :], in_=half_norm[rows, 0:n], axis=AXIS.X, op=ALU.max, negate=True)
+            return a
 
         def p_of(m, cut=slice(0, O)):
             return p_all[:, m, cut]
 
-        def pair(name, a, b, op):
-            r = column(name)
-            nc.vector.tensor_tensor(out=r[:], in0=a[:], in1=b[:], op=op)
-            return r
+        def pair(out, rows, a, b, op):
+            nc.vector.tensor_tensor(out=out[rows, :], in0=a[rows, :], in1=b[rows, :], op=op)
+            return out
 
-        neg_max1 = column("neg_max1")
-        d1, r1, d2, r2, d3, r3, uS, rS = [wide(n) for n in ("d1", "r1", "d2", "r2", "d3", "r3", "uS", "rS")]
-        A, B = CUTS
+        d1, r1, d2, r2, u, last = [wide(n) for n in ("d1", "r1", "d2", "r2", "u", "last")]
+        share = column("share")
         add_b2(3)
         root(half_norm[:, 1:2], 1, 2, both)
-        t1 = tanh("t1", 0, half_norm[:, 1:2], -1.0)
+        t1 = tanh("t1", both, 0, half_norm[:, 1:2], -1.0)
         square(3)
         root(half_norm[:, 2:3], 2, 3, both)
         minus(d1[:], p_of(1), p_of(0))
-        negmax(neg_max1[:], both, 2)
-        w1 = affine("w1", t1, 0.5, 0.5)
+        neg_max1 = negmax("neg_max1", both, 2)
+        w1 = affine("w1", both, t1, 0.5, 0.5)
         add_b2(4)
         a1 = column("a1")
         nc.scalar.activation(out=a1[:], in_=t1[:], func=ACT.Abs)
-        aa = line("aa", a1, 1.0, plus_one)
-        am = line("am", a1, 1.0, minus_one)
-        ap = line("ap", a1, 1.0, plus_three)
-        t2 = tanh("t2", 2, neg_max1[:])
+        aa = line(column("aa"), both, a1, 1.0, plus_one)
+        am = line(column("am"), both, a1, 1.0, minus_one)
+        ap = line(column("ap"), both, a1, 1.0, plus_three)
+        t2 = tanh("t2", both, 2, neg_max1[:])
         square(4)
+        store(nc.sync, 0, high, p_of(4))
         root(half_norm[:, 3:4], 3, 4, both)
-        root(short_bias[low, :], 4, 5, low)
+        root(half_norm[low, 4:5], 4, 5, low)
         for cut in CUTS:
             weigh(r1[:, cut], d1[:, cut], w1, p_of(0, cut))
-        negmax(long_bias[high, :], high, 3)
-        t3 = tanh("t3", 3, long_bias[:])
-        tS = tanh("tS", 3, short_bias[:], -1.0)
-        vS = line("vS", tS, -0.5, half)
-        wS = line("wS", tS, 0.5, half)
-        den2 = affine("den2", t2, am[:], ap[:])
-        num2 = plus_one_times("num2", t2, aa)
+        neg_max2 = negmax("neg_max2", high, 3)
+        den2 = affine("den2", both, t2, am[:], ap[:])
+        num2 = plus_one_times("num2", both, t2, aa)
         abs2 = magnitude("abs2", t2)
         minus(d2[:, A], p_of(2, A), r1[:, A])
-        rden2 = reciprocal("rden2", den2)
-        a2 = plus_one_times("a2", abs2, aa)
+        rden2 = reciprocal("rden2", both, den2)
+        a2 = plus_one_times("a2", both, abs2, aa)
         minus(d2[:, B], p_of(2, B), r1[:, B])
-        w2 = pair("w2", num2, rden2, ALU.mult)
-        am2 = pair("am2", a2, den2, ALU.subtract)
-        ap2 = pair("ap2", a2, den2, ALU.add)
-        num3 = plus_one_times("num3", t3, a2)
-        den3 = affine("den3", t3, am2[:], ap2[:])
+        w2 = pair(column("w2"), both, num2, rden2, ALU.mult)
+        am2 = pair(column("am2"), both, a2, den2, ALU.subtract)
+        ap2 = pair(column("ap2"), both, a2, den2, ALU.add)
+        t3 = tanh("t3", high, 3, neg_max2[high, :])
+        tS = tanh("tS", low, 4, half_norm[low, 3:4], -1.0)
+        vS = line(column("vS"), low, tS, -0.5, half)
+        line(share, low, tS, 0.5, half)
+        for cut in CUTS:
+            nc.scalar.activation(out=u[low, cut], in_=p_all[low, 4, cut], func=ACT.Copy, scale=vS[low, :])
+        num3 = plus_one_times("num3", high, t3, a2)
+        den3 = affine("den3", high, t3, am2[high, :], ap2[high, :])
         weigh(r2[:, A], d2[:, A], w2, r1[:, A])
-        rden3 = reciprocal("rden3", den3)
+        rden3 = reciprocal("rden3", high, den3)
+        rest3 = pair(column("rest3"), high, den3, num3, ALU.subtract)
         weigh(r2[:, B], d2[:, B], w2, r1[:, B])
-        w3 = pair("w3", num3, rden3, ALU.mult)
+        store(nc.sync, 2, low, r2)
+        pair(share, high, num3, rden3, ALU.mult)
         for cut in CUTS:
-            minus(d3[:, cut], p_of(3, cut), r2[:, cut])
+            nc.vector.tensor_scalar(
+                out=u[high, cut], in0=r2[high, cut], scalar1=rest3[high, :], scalar2=rden3[high, :], op0=ALU.mult, op1=ALU.mult
+            )
         for cut in CUTS:
-            nc.scalar.activation(out=uS[:, cut], in_=p_of(3, cut), func=ACT.Copy, scale=vS[:])
-        for cut in CUTS:
-            weigh(r3[:, cut], d3[:, cut], w3, r2[:, cut])
-        store(LONG, r3, nc.sync)
-        for cut in CUTS:
-            weigh(rS[:, cut], p_of(4, cut), wS, uS[:, cut])
-        store(SHORT, rS, nc.scalar)
+            weigh(last[:, cut], p_of(3, cut), share, u[:, cut])
+        store(nc.sync, 3, high, last)
+        store(nc.scalar, 1, low, last)

@@ -6,7 +6,6 @@ import concourse.mybir as mybir
 F32 = mybir.dt.float32
 BF16 = mybir.dt.bfloat16
 U32 = mybir.dt.uint32
-I32 = mybir.dt.int32
 U8 = mybir.dt.uint8
 FP8X4 = mybir.dt.float8_e4m3fn_x4
 ACT = mybir.ActivationFunctionType
@@ -173,13 +172,13 @@ def tile_pairconnect_s_kernel(tc, x, W1, b1, W2, b2, out):
         regroup_w1(nc.scalar.copy, 1, scalar_cols)
         quantise_w1(0)
         quantise_w1(1)
-        def duplicate_blocks():
+        def extras():
             for block in range(len(BLOCK_ORDER)):
                 if not RUN_AT <= block < RUN_AT + POSITIONS:
-                    src = slice((RUN_AT + BLOCK_ORDER[block]) * HALF, (RUN_AT + BLOCK_ORDER[block] + 1) * HALF)
-                    dst = slice(block * HALF, (block + 1) * HALF)
-                    nc.sync.dma_start(out=x_codes[:, dst].bitcast(I32), in_=x_codes[:, src].bitcast(I32))
-                    nc.sync.dma_start(out=x_scales[:, dst], in_=x_scales[:, src])
+                    for g in range(2):
+                        nc.scalar.copy(
+                            out=x_grouped_words[:, g, block], in_=x_t_by_position[g][:, BLOCK_ORDER[block]]
+                        )
 
         w2_grouped = keep.tile([P, O, PACK], BF16, align_bytes=64)
         w2_codes = keep.tile([P, O], U32, align_bytes=64)
@@ -303,7 +302,9 @@ def tile_pairconnect_s_kernel(tc, x, W1, b1, W2, b2, out):
 
         regroup_w2(nc.vector.tensor_copy, 0, 256)
         regroup_w2(nc.scalar.copy, 256, 384)
-        duplicate_blocks()
+        extras()
+        quantise_x(0, RUN_AT)
+        quantise_x(RUN_AT + POSITIONS, len(BLOCK_ORDER) - RUN_AT - POSITIONS)
         quantise_w2(0)
         stage1_spread()
         add_b1_and_gelu(0)

@@ -351,9 +351,9 @@ def tile_pairconnect_s_kernel(tc, x, W1, b1, W2, b2, out):
         CUTS = (slice(0, O // 2), slice(O // 2, O))
         A, B = CUTS
 
-        def tanh(name, rows, n, bias, scale=1.0):
+        def tanh(name, n, bias, scale=1.0):
             t = column(name)
-            nc.scalar.activation(out=t[rows, :], in_=half_norm[rows, n : n + 1], func=ACT.Tanh, bias=bias, scale=scale)
+            nc.scalar.activation(out=t[:], in_=half_norm[:, n : n + 1], func=ACT.Tanh, bias=bias, scale=scale)
             return t
 
         def minus(out, a, b):
@@ -362,9 +362,9 @@ def tile_pairconnect_s_kernel(tc, x, W1, b1, W2, b2, out):
         def weigh(out, part, weight, rest):
             nc.vector.scalar_tensor_tensor(out=out, in0=part, scalar=weight[:], in1=rest, op0=ALU.mult, op1=ALU.add)
 
-        def affine(name, rows, t, mult, add):
+        def affine(name, t, mult, add):
             a = column(name)
-            nc.vector.tensor_scalar(out=a[rows, :], in0=t[rows, :], scalar1=mult, scalar2=add, op0=ALU.mult, op1=ALU.add)
+            nc.vector.tensor_scalar(out=a[:], in0=t[:], scalar1=mult, scalar2=add, op0=ALU.mult, op1=ALU.add)
             return a
 
         def magnitude(name, t):
@@ -372,85 +372,88 @@ def tile_pairconnect_s_kernel(tc, x, W1, b1, W2, b2, out):
             nc.vector.scalar_tensor_tensor(out=a[:], in0=t[:], scalar=-1.0, in1=t[:], op0=ALU.mult, op1=ALU.max)
             return a
 
-        def plus_one_times(name, rows, t, factor):
+        def plus_one_times(name, t, factor):
             a = column(name)
-            nc.vector.scalar_tensor_tensor(out=a[rows, :], in0=t[rows, :], scalar=1.0, in1=factor[rows, :], op0=ALU.add, op1=ALU.mult)
+            nc.vector.scalar_tensor_tensor(out=a[:], in0=t[:], scalar=1.0, in1=factor[:], op0=ALU.add, op1=ALU.mult)
             return a
 
-        def reciprocal(name, rows, t):
+        def reciprocal(name, t):
             a = column(name)
-            nc.vector.reciprocal(out=a[rows, :], in_=t[rows, :])
+            nc.vector.reciprocal(out=a[:], in_=t[:])
             return a
 
-        def line(out, rows, t, scale, bias):
-            nc.scalar.activation(out=out[rows, :], in_=t[rows, :], func=ACT.Identity, scale=scale, bias=bias[rows, :])
-            return out
-
-        def negmax(name, rows, n):
+        def line(name, t, scale, bias):
             a = column(name)
-            nc.vector.tensor_reduce(out=a[rows, :], in_=half_norm[rows, 0:n], axis=AXIS.X, op=ALU.max, negate=True)
+            nc.scalar.activation(out=a[:], in_=t[:], func=ACT.Identity, scale=scale, bias=bias)
+            return a
+
+        def negmax(name, n):
+            a = column(name)
+            nc.vector.tensor_reduce(out=a[:], in_=half_norm[:, 0:n], axis=AXIS.X, op=ALU.max, negate=True)
             return a
 
         def p_of(m, cut=slice(0, O)):
             return p_all[:, m, cut]
 
-        def pair(out, rows, a, b, op):
-            nc.vector.tensor_tensor(out=out[rows, :], in0=a[rows, :], in1=b[rows, :], op=op)
-            return out
+        def pair(name, a, b, op):
+            r = column(name)
+            nc.vector.tensor_tensor(out=r[:], in0=a[:], in1=b[:], op=op)
+            return r
 
-        d1, r1, d2, r2, u, last = [wide(n) for n in ("d1", "r1", "d2", "r2", "u", "last")]
-        share = column("share")
+        d1, r1, d2, r2, u3, r3, uS, rS = [wide(n) for n in ("d1", "r1", "d2", "r2", "u3", "r3", "uS", "rS")]
         add_b2(3)
         root(half_norm[:, 1:2], 1, 2, both)
-        t1 = tanh("t1", both, 0, half_norm[:, 1:2], -1.0)
+        t1 = tanh("t1", 0, half_norm[:, 1:2], -1.0)
         square(3)
         root(half_norm[:, 2:3], 2, 3, both)
         minus(d1[:], p_of(1), p_of(0))
-        neg_max1 = negmax("neg_max1", both, 2)
-        w1 = affine("w1", both, t1, 0.5, 0.5)
+        neg_max1 = negmax("neg_max1", 2)
+        w1 = affine("w1", t1, 0.5, 0.5)
         add_b2(4)
         a1 = column("a1")
         nc.scalar.activation(out=a1[:], in_=t1[:], func=ACT.Abs)
-        aa = line(column("aa"), both, a1, 1.0, plus_one)
-        am = line(column("am"), both, a1, 1.0, minus_one)
-        ap = line(column("ap"), both, a1, 1.0, plus_three)
-        t2 = tanh("t2", both, 2, neg_max1[:])
+        aa = line("aa", a1, 1.0, plus_one)
+        am = line("am", a1, 1.0, minus_one)
+        ap = line("ap", a1, 1.0, plus_three)
+        t2 = tanh("t2", 2, neg_max1[:])
         square(4)
         store(nc.sync, 0, high, p_of(4))
         root(half_norm[:, 3:4], 3, 4, both)
-        root(half_norm[low, 4:5], 4, 5, low)
+        root(half_norm[:, 4:5], 4, 5, both)
         for cut in CUTS:
             weigh(r1[:, cut], d1[:, cut], w1, p_of(0, cut))
-        neg_max2 = negmax("neg_max2", high, 3)
-        den2 = affine("den2", both, t2, am[:], ap[:])
-        num2 = plus_one_times("num2", both, t2, aa)
+        neg_max2 = negmax("neg_max2", 3)
+        den2 = affine("den2", t2, am[:], ap[:])
+        num2 = plus_one_times("num2", t2, aa)
         abs2 = magnitude("abs2", t2)
         minus(d2[:, A], p_of(2, A), r1[:, A])
-        rden2 = reciprocal("rden2", both, den2)
-        a2 = plus_one_times("a2", both, abs2, aa)
+        rden2 = reciprocal("rden2", den2)
+        a2 = plus_one_times("a2", abs2, aa)
         minus(d2[:, B], p_of(2, B), r1[:, B])
-        w2 = pair(column("w2"), both, num2, rden2, ALU.mult)
-        am2 = pair(column("am2"), both, a2, den2, ALU.subtract)
-        ap2 = pair(column("ap2"), both, a2, den2, ALU.add)
-        t3 = tanh("t3", high, 3, neg_max2[high, :])
-        tS = tanh("tS", low, 4, half_norm[low, 3:4], -1.0)
-        vS = line(column("vS"), low, tS, -0.5, half)
-        line(share, low, tS, 0.5, half)
+        w2 = pair("w2", num2, rden2, ALU.mult)
+        am2 = pair("am2", a2, den2, ALU.subtract)
+        ap2 = pair("ap2", a2, den2, ALU.add)
+        t3 = tanh("t3", 3, neg_max2[:])
+        tS = tanh("tS", 4, half_norm[:, 3:4], -1.0)
+        vS = line("vS", tS, -0.5, half)
+        wS = line("wS", tS, 0.5, half)
         for cut in CUTS:
-            nc.scalar.activation(out=u[low, cut], in_=p_all[low, 4, cut], func=ACT.Copy, scale=vS[low, :])
-        num3 = plus_one_times("num3", high, t3, a2)
-        den3 = affine("den3", high, t3, am2[high, :], ap2[high, :])
+            nc.scalar.activation(out=uS[:, cut], in_=p_of(4, cut), func=ACT.Copy, scale=vS[:])
+        num3 = plus_one_times("num3", t3, a2)
+        den3 = affine("den3", t3, am2[:], ap2[:])
         weigh(r2[:, A], d2[:, A], w2, r1[:, A])
-        rden3 = reciprocal("rden3", high, den3)
-        rest3 = pair(column("rest3"), high, den3, num3, ALU.subtract)
+        rden3 = reciprocal("rden3", den3)
+        rest3 = pair("rest3", den3, num3, ALU.subtract)
         weigh(r2[:, B], d2[:, B], w2, r1[:, B])
         store(nc.sync, 2, low, r2)
-        pair(share, high, num3, rden3, ALU.mult)
+        w3 = pair("w3", num3, rden3, ALU.mult)
         for cut in CUTS:
             nc.vector.tensor_scalar(
-                out=u[high, cut], in0=r2[high, cut], scalar1=rest3[high, :], scalar2=rden3[high, :], op0=ALU.mult, op1=ALU.mult
+                out=u3[:, cut], in0=r2[:, cut], scalar1=rest3[:], scalar2=rden3[:], op0=ALU.mult, op1=ALU.mult
             )
         for cut in CUTS:
-            weigh(last[:, cut], p_of(3, cut), share, u[:, cut])
-        store(nc.sync, 3, high, last)
-        store(nc.scalar, 1, low, last)
+            weigh(r3[:, cut], p_of(3, cut), w3, u3[:, cut])
+        store(nc.sync, 3, high, r3)
+        for cut in CUTS:
+            weigh(rS[:, cut], p_of(3, cut), wS, uS[:, cut])
+        store(nc.scalar, 1, low, rS)

@@ -65,9 +65,6 @@ def tile_pairconnect_s_kernel(tc, x, W1, b1, W2, b2, out):
         banks = ctx.enter_context(tc.psum_pool(name="banks", bufs=1))
         ctx.enter_context(tc.manual_schedule())
 
-        b2_row = keep.tile([P, O], BF16)
-        nc.vector.memset(b2_row[:], 0.0)
-        nc.scalar.dma_start(out=b2_row[0:1, :], in_=b2.unsqueeze(0))
         b1_bf = keep.tile([P, PACK], BF16)
         nc.scalar.dma_start(out=b1_bf[:], in_=b1.rearrange("(q t) -> q t", t=PACK))
 
@@ -84,9 +81,11 @@ def tile_pairconnect_s_kernel(tc, x, W1, b1, W2, b2, out):
             )
         w2_rows = keep.tile([P, PACK, O], BF16)
         nc.sync.dma_start(out=w2_rows[:], in_=W2.rearrange("(p j) o -> p j o", j=PACK))
-        ones = keep.tile([P, P], BF16)
-        nc.vector.memset(ones[:], 1.0)
+        b2_all = keep.tile([P, O], BF16)
+        nc.sync.dma_start(out=b2_all[:], in_=b2.partition_broadcast(P))
 
+        wide_ones = keep.tile([P, 512], BF16)
+        nc.vector.memset(wide_ones[:], 1.0)
         zero = keep.tile([P, 1], F32)
         nc.vector.memset(zero[:], 0.0)
         warm = keep.tile([P, 1], F32)
@@ -131,12 +130,11 @@ def tile_pairconnect_s_kernel(tc, x, W1, b1, W2, b2, out):
             )
 
 
-        b2_ps = banks.tile([P, O], F32, name="bank2")
-        nc.tensor.matmul(out=b2_ps[:], lhsT=ones[:], rhs=b2_row[:], start=True, stop=True)
-        b2_all = keep.tile([P, O], F32)
-
-        def b2_copy():
-            nc.scalar.copy(out=b2_all[:], in_=b2_ps[:])
+        dummy = banks.tile([P, 512], F32, name="bank7")
+        for k in range(3):
+            nc.tensor.matmul(
+                out=dummy[:], lhsT=wide_ones[:, 0:P], rhs=wide_ones[:], start=True, stop=True
+            )
 
         w1_grouped = keep.tile([P, 2 * PACK * F], BF16, align_bytes=64)
         w1_grouped_view = w1_grouped[:].rearrange(
@@ -308,7 +306,6 @@ def tile_pairconnect_s_kernel(tc, x, W1, b1, W2, b2, out):
         quantise_w2(0)
         stage1_spread()
         add_b1_and_gelu(0)
-        b2_copy()
         stage1(1, 7)
         add_b1_and_gelu(1)
         quantise_w2(1)

@@ -65,13 +65,9 @@ def tile_pairconnect_s_kernel(tc, x, W1, b1, W2, b2, out):
         banks = ctx.enter_context(tc.psum_pool(name="banks", bufs=1))
         ctx.enter_context(tc.manual_schedule())
 
-        b1_bf = keep.tile([P, PACK], BF16)
-        nc.scalar.dma_start(out=b1_bf[:], in_=b1.rearrange("(q t) -> q t", t=PACK))
-
         x_rows = keep.tile([P, 2 * D], BF16)
         nc.sync.dma_start(
-            out=x_rows[:].rearrange("r (g k) -> r g k", g=2),
-            in_=x.flatten_outer_dims().rearrange("(g r) k -> r g k", r=P),
+            out=x_rows[:], in_=x.flatten_outer_dims().rearrange("(r g) k -> r (g k)", g=2)
         )
         w1_rows = keep.tile([P, 2, PACK, F], BF16)
         for half in range(2):
@@ -81,6 +77,8 @@ def tile_pairconnect_s_kernel(tc, x, W1, b1, W2, b2, out):
             )
         w2_rows = keep.tile([P, PACK, O], BF16)
         nc.sync.dma_start(out=w2_rows[:], in_=W2.rearrange("(p j) o -> p j o", j=PACK))
+        b1_bf = keep.tile([P, PACK], BF16)
+        nc.sync.dma_start(out=b1_bf[:], in_=b1.rearrange("(q t) -> q t", t=PACK))
         b2_all = keep.tile([P, O], BF16)
         nc.sync.dma_start(out=b2_all[:], in_=b2.partition_broadcast(P))
 
@@ -113,11 +111,9 @@ def tile_pairconnect_s_kernel(tc, x, W1, b1, W2, b2, out):
                 )
         x_grouped = keep.tile([P, X_COLS * PACK], BF16, align_bytes=64)
         x_grouped_words = x_grouped[:].bitcast(F32).rearrange(
-            "p (s g b u) -> p g s b u", s=len(BLOCK_ORDER), g=2, u=2
+            "p (s b u) -> p s b u", s=len(BLOCK_ORDER), u=2
         )
-        x_t_by_position = [
-            tile[:].rearrange("p u (b i) -> p i b u", i=POSITIONS) for tile in x_t
-        ]
+        x_by_slot = [tile[:].rearrange("p u (b h) -> p h b u", h=2) for tile in x_t]
         x_codes = keep.tile([P, X_COLS], U32, align_bytes=64)
         x_scales = keep.tile([P, X_COLS], U8, align_bytes=64)
 
@@ -160,9 +156,10 @@ def tile_pairconnect_s_kernel(tc, x, W1, b1, W2, b2, out):
 
         vector_cols = slice(0, W1_VECTOR_COLS)
         scalar_cols = slice(W1_VECTOR_COLS, P)
-        run = slice(RUN_AT, RUN_AT + POSITIONS)
         for g in range(2):
-            nc.scalar.copy(out=x_grouped_words[:, g, run], in_=x_t_by_position[g])
+            nc.scalar.copy(
+                out=x_grouped_words[:, RUN_AT + g : RUN_AT + POSITIONS : 2], in_=x_by_slot[g]
+            )
         regroup_w1(nc.vector.tensor_copy, 0, vector_cols)
         regroup_w1(nc.scalar.copy, 0, scalar_cols)
         quantise_x(RUN_AT, POSITIONS)
@@ -173,10 +170,8 @@ def tile_pairconnect_s_kernel(tc, x, W1, b1, W2, b2, out):
         def extras():
             for block in range(len(BLOCK_ORDER)):
                 if not RUN_AT <= block < RUN_AT + POSITIONS:
-                    for g in range(2):
-                        nc.scalar.copy(
-                            out=x_grouped_words[:, g, block], in_=x_t_by_position[g][:, BLOCK_ORDER[block]]
-                        )
+                    h, g = divmod(BLOCK_ORDER[block], 2)
+                    nc.scalar.copy(out=x_grouped_words[:, block], in_=x_by_slot[g][:, h])
 
         w2_grouped = keep.tile([P, O, PACK], BF16, align_bytes=64)
         w2_codes = keep.tile([P, O], U32, align_bytes=64)

from contextlib import ExitStack

import concourse.masks as masks
import concourse.mybir as mybir

F32 = mybir.dt.float32
BF16 = mybir.dt.bfloat16
U32 = mybir.dt.uint32
U8 = mybir.dt.uint8
FP8X4 = mybir.dt.float8_e4m3fn_x4
ACT = mybir.ActivationFunctionType
ALU = mybir.AluOpType
AXIS = mybir.AxisListType

BATCH, POSITIONS, D, F, O = 64, 4, 512, 512, 384
P = 128
PACK = 4
HALF = 64
NEG = -1e9

FLOPS = 2 * BATCH * POSITIONS * 2 * D * F + 2 * BATCH * 10 * F * O

PAIRS = (
    ((2, 0), (3, 1)),
    ((2, 1), (3, 2)),
    ((2, 2), (3, 3)),
    ((1, 1), (3, 0)),
    ((1, 0), (0, 0)),
)
TILES = len(PAIRS)
ROWS_OF_RESULT = ((2, 3), (1, 0))
LONG, SHORT = 0, 1
BLOCK_ORDER = (1, 0, 0, 1, 2, 3, 1, 3)
RUN_AT = 2
X_COLS = len(BLOCK_ORDER) * HALF

W1_VECTOR_COLS = 80
Q_BANKS = (2, 4, 5, 6, 7)
PRE_AHEAD = 3


def first_block(low, high):
    for block in range(len(BLOCK_ORDER) - 1):
        if BLOCK_ORDER[block] == low and BLOCK_ORDER[block + 1] == high:
            return block
    raise ValueError("BLOCK_ORDER lacks a pair of positions")


def result_of(m, side):
    for a in range(2):
        if ROWS_OF_RESULT[a][side] == PAIRS[m][side][0]:
            return a
    raise ValueError("ROWS_OF_RESULT lacks an output row")


def tiles_of_result(a):
    tiles = [m for m in range(TILES) if a in (result_of(m, 0), result_of(m, 1))]
    return tiles[0], tiles[-1] + 1


def tile_pairconnect_s_kernel(tc, x, W1, b1, W2, b2, out):
    nc = tc.nc
    with ExitStack() as ctx:
        keep = ctx.enter_context(tc.tile_pool(name="keep", bufs=1))
        banks = ctx.enter_context(tc.psum_pool(name="banks", bufs=1))
        ctx.enter_context(tc.manual_schedule())

        x_rows = keep.tile([P, 2 * D], BF16)
        nc.sync.dma_start(
            out=x_rows[:], in_=x.flatten_outer_dims().rearrange("(r g) k -> r (g k)", g=2)
        )
        w1_rows = keep.tile([P, 2, PACK, F], BF16)
        for half in range(2):
            nc.sync.dma_start(
                out=w1_rows[:, half],
                in_=W1[half * D : (half + 1) * D, :].rearrange("(p j) f -> p j f", j=PACK),
            )
        w2_rows = keep.tile([P, PACK, O], BF16)
        nc.sync.dma_start(out=w2_rows[:], in_=W2.rearrange("(p j) o -> p j o", j=PACK))
        b1_bf = keep.tile([P, PACK], BF16)
        nc.sync.dma_start(out=b1_bf[:], in_=b1.rearrange("(q t) -> q t", t=PACK))
        b2_all = keep.tile([P, O], BF16)
        nc.sync.dma_start(out=b2_all[:], in_=b2.partition_broadcast(P))

        wide_ones = keep.tile([P, 512], BF16)
        nc.vector.memset(wide_ones[:], 1.0)
        zero = keep.tile([P, 1], F32)
        nc.vector.memset(zero[:], 0.0)
        warm = keep.tile([P, 1], F32)
        nc.scalar.activation(out=warm[:], in_=zero[:], func=ACT.Gelu)

        ident = keep.tile([P, P], F32)
        masks.make_identity(nc, ident[:])
        half_power = keep.tile([P, TILES], F32)
        nc.gpsimd.memset(half_power[:], 0.5)
        def constant(name, value):
            c = keep.tile([P, 1], F32, name=name)
            nc.gpsimd.memset(c[:], value)
            return c[:]

        half = half_power[:, 0:1]
        plus_one, minus_one, plus_three = constant("c1", 1.0), constant("cm1", -1.0), constant("c3", 3.0)

        x_words = x_rows[:].bitcast(F32).rearrange("r (g p u) -> r g u p", g=2, u=2)
        x_t = []
        for g in range(2):
            x_t.append(banks.tile([P, 2, P], F32, name="bank%d" % g))
            for u in range(2):
                nc.tensor.transpose(
                    out=x_t[g][:, u, :], in_=x_words[:, g, u, :], identity=ident[:]
                )
        x_grouped = keep.tile([P, X_COLS * PACK], BF16, align_bytes=64)
        x_grouped_words = x_grouped[:].bitcast(F32).rearrange(
            "p (s b u) -> p s b u", s=len(BLOCK_ORDER), u=2
        )
        x_by_slot = [tile[:].rearrange("p u (b h) -> p h b u", h=2) for tile in x_t]
        x_codes = keep.tile([P, X_COLS], U32, align_bytes=64)
        x_scales = keep.tile([P, X_COLS], U8, align_bytes=64)

        def quantise_x(first, blocks):
            cols = slice(first * HALF, (first + blocks) * HALF)
            nc.vector.quantize_mx(
                out=x_codes[:, cols].bitcast(FP8X4),
                scales=x_scales[:, cols],
                in_=x_grouped[:, first * HALF * PACK : (first + blocks) * HALF * PACK],
            )


        dummy = banks.tile([P, 512], F32, name="bank7")
        for k in range(3):
            nc.tensor.matmul(
                out=dummy[:], lhsT=wide_ones[:, 0:P], rhs=wide_ones[:], start=True, stop=True
            )

        w1_grouped = keep.tile([P, 2 * PACK * F], BF16, align_bytes=64)
        w1_grouped_view = w1_grouped[:].rearrange(
            "p (h t q j) -> p h t q j", h=2, t=PACK, j=PACK
        )
        w1_codes = keep.tile([P, 2 * F], U32, align_bytes=64)
        w1_scales = keep.tile([P, 2 * F], U8, align_bytes=64)

        def regroup_w1(copy, half, cols):
            copy(
                out=w1_grouped_view[:, half, :, cols, :].rearrange("p t q j -> p q j t"),
                in_=w1_rows[:, half].rearrange("p j (q t) -> p q j t", t=PACK)[:, cols],
            )

        def quantise_w1(half):
            for part in range(2 * half, 2 * half + 2):
                cols = slice(part * F // 2, (part + 1) * F // 2)
                nc.vector.quantize_mx(
                    out=w1_codes[:, cols].bitcast(FP8X4),
                    scales=w1_scales[:, cols],
                    in_=w1_grouped[:, part * PACK * F // 2 : (part + 1) * PACK * F // 2],
                )

        vector_cols = slice(0, W1_VECTOR_COLS)
        scalar_cols = slice(W1_VECTOR_COLS, P)
        for g in range(2):
            nc.scalar.copy(
                out=x_grouped_words[:, RUN_AT + g : RUN_AT + POSITIONS : 2], in_=x_by_slot[g]
            )
        regroup_w1(nc.vector.tensor_copy, 0, vector_cols)
        regroup_w1(nc.scalar.copy, 0, scalar_cols)
        quantise_x(RUN_AT, POSITIONS)
        regroup_w1(nc.vector.tensor_copy, 1, vector_cols)
        regroup_w1(nc.scalar.copy, 1, scalar_cols)
        quantise_w1(0)
        quantise_w1(1)
        def extras():
            for block in range(len(BLOCK_ORDER)):
                if not RUN_AT <= block < RUN_AT + POSITIONS:
                    h, g = divmod(BLOCK_ORDER[block], 2)
                    nc.scalar.copy(out=x_grouped_words[:, block], in_=x_by_slot[g][:, h])

        w2_grouped = keep.tile([P, O, PACK], BF16, align_bytes=64)
        w2_codes = keep.tile([P, O], U32, align_bytes=64)
        w2_scales = keep.tile([P, O], U8, align_bytes=64)
        w2_parts = ((0, 256), (256, 384))

        def regroup_w2(copy, lo, hi):
            copy(
                out=w2_grouped[:, lo:hi].rearrange("p (c i) j -> p c j i", i=4),
                in_=w2_rows[:, :, lo:hi].rearrange("p j (c i) -> p c j i", i=4),
            )

        def quantise_w2(part):
            flat = w2_grouped[:].rearrange("p o j -> p (o j)")
            for lo, hi in w2_parts[part:part+1]:
                nc.vector.quantize_mx(
                    out=w2_codes[:, lo:hi].bitcast(FP8X4),
                    scales=w2_scales[:, lo:hi],
                    in_=flat[:, lo * PACK : hi * PACK],
                )

        h_chunks = keep.tile([P, TILES, PACK, P], BF16)
        h_grouped = keep.tile([P, TILES, P * PACK], BF16, align_bytes=64)
        h_codes = keep.tile([P, TILES, P], U32, align_bytes=64)
        h_scales = keep.tile([P, TILES, P], U8, align_bytes=64)
        p_all = keep.tile([P, TILES, O], F32)
        p_squared = keep.tile([P, TILES, O], F32)
        quarter_norm2 = keep.tile([P, TILES], F32)
        half_norm = keep.tile([P, TILES], F32)
        pre_tiles = {}
        q_tiles = {}

        def x_start(m, half):
            (i_low, j_low), (i_high, j_high) = PAIRS[m]
            low, high = ((i_low, i_high), (j_low, j_high))[half]
            return first_block(low, high) * HALF

        def stage1_pass(m, t, half):
            w_cols = slice((half * PACK + t) * P, (half * PACK + t + 1) * P)
            x_cols = slice(x_start(m, half), x_start(m, half) + P)
            nc.tensor.matmul_mx(
                out=pre_tiles[m, t],
                lhsT=w1_codes[:, w_cols].bitcast(FP8X4),
                lhsT_scale=w1_scales[:, w_cols],
                rhs=x_codes[:, x_cols].bitcast(FP8X4),
                rhs_scale=x_scales[:, x_cols],
                start=(half == 0),
                stop=(half == 1),
            )

        def stage1_spread():
            for t in range(PACK):
                pre = banks.tile([P, P], F32, name="bank%d" % (3 + t))
                pre_tiles[0, t] = pre[:]
            for half in range(2):
                for t in range(PACK):
                    stage1_pass(0, t, half)

        def stage1(m, bank):
            pre = banks.tile([P, PACK, P], F32, name="bank%d" % bank)
            for t in range(PACK):
                pre_tiles[m, t] = pre[:, t, :]
                for half in range(2):
                    stage1_pass(m, t, half)

        def add_b1_and_gelu(m):
            for t in range(PACK):
                nc.scalar.activation(
                    out=h_chunks[:, m, t, :],
                    in_=pre_tiles[m, t],
                    func=ACT.Gelu,
                    bias=b1_bf[:, t : t + 1],
                )

        def group_h(m, copy=nc.vector.tensor_copy):
            copy(
                out=h_grouped[:, m].rearrange("q (c i t) -> q c t i", i=4, t=PACK),
                in_=h_chunks[:, m].rearrange("q t (c i) -> q c t i", i=4),
            )

        def quantise_h_and_stage2(m):
            nc.vector.quantize_mx(
                out=h_codes[:, m, :].bitcast(FP8X4), scales=h_scales[:, m, :], in_=h_grouped[:, m]
            )
            q = banks.tile([P, O], F32, name="bank%d" % Q_BANKS[m])
            q_tiles[m] = q
            for lo, hi in w2_parts:
                nc.tensor.matmul_mx(
                    out=q[:, lo:hi],
                    lhsT=h_codes[:, m, :].bitcast(FP8X4),
                    lhsT_scale=h_scales[:, m, :],
                    rhs=w2_codes[:, lo:hi].bitcast(FP8X4),
                    rhs_scale=w2_scales[:, lo:hi],
                    start=True,
                    stop=True,
                )

        def add_b2(m):
            nc.vector.tensor_tensor(
                out=p_all[:, m, :], in0=q_tiles[m][:], in1=b2_all[:], op=ALU.add
            )

        def square(m):
            nc.scalar.activation(
                out=p_squared[:, m, :],
                in_=p_all[:, m, :],
                func=ACT.Square,
                scale=0.5,
                accum_out=quarter_norm2[:, m : m + 1],
            )

        def root(out, lo, hi, rows):
            nc.gpsimd.tensor_tensor(
                out=out,
                in0=quarter_norm2[rows, lo:hi],
                in1=half_power[rows, 0 : hi - lo],
                op=ALU.pow,
            )

        low, high, both = slice(0, HALF), slice(HALF, P), slice(0, P)

        regroup_w2(nc.vector.tensor_copy, 0, 256)
        regroup_w2(nc.scalar.copy, 256, 384)
        extras()
        quantise_x(0, RUN_AT)
        quantise_x(RUN_AT + POSITIONS, len(BLOCK_ORDER) - RUN_AT - POSITIONS)
        quantise_w2(0)
        stage1_spread()
        add_b1_and_gelu(0)
        stage1(1, 7)
        add_b1_and_gelu(1)
        quantise_w2(1)
        group_h(0)
        stage1(2, 0)
        add_b1_and_gelu(2)
        stage1(3, 1)
        quantise_h_and_stage2(0)
        add_b1_and_gelu(3)
        stage1(4, 3)
        group_h(1)
        quantise_h_and_stage2(1)
        add_b1_and_gelu(4)
        group_h(2)
        add_b2(0)
        square(0)
        quantise_h_and_stage2(2)

        group_h(3)
        add_b2(1)
        square(1)

        quantise_h_and_stage2(3)
        group_h(4)
        add_b2(2)
        square(2)
        quantise_h_and_stage2(4)
        root(half_norm[:, 0:1], 0, 1, both)
        out_by_row = out.rearrange("b i o -> i b o")

        def store(queue, i, rows, result):
            queue.dma_start(out=out_by_row[i], in_=result[rows, :])

        def column(name):
            return keep.tile([P, 1], F32, name=name)

        def wide(name):
            return keep.tile([P, O], F32, name=name)

        CUTS = (slice(0, O // 2), slice(O // 2, O))
        A, B = CUTS

        def tanh(name, n, bias, scale=1.0):
            t = column(name)
            nc.scalar.activation(out=t[:], in_=half_norm[:, n : n + 1], func=ACT.Tanh, bias=bias, scale=scale)
            return t

        def minus(out, a, b):
            nc.vector.tensor_tensor(out=out, in0=a, in1=b, op=ALU.subtract)

        def weigh(out, part, weight, rest):
            nc.vector.scalar_tensor_tensor(out=out, in0=part, scalar=weight[:], in1=rest, op0=ALU.mult, op1=ALU.add)

        def affine(name, t, mult, add):
            a = column(name)
            nc.vector.tensor_scalar(out=a[:], in0=t[:], scalar1=mult, scalar2=add, op0=ALU.mult, op1=ALU.add)
            return a

        def magnitude(name, t):
            a = column(name)
            nc.vector.scalar_tensor_tensor(out=a[:], in0=t[:], scalar=-1.0, in1=t[:], op0=ALU.mult, op1=ALU.max)
            return a

        def plus_one_times(name, t, factor):
            a = column(name)
            nc.vector.scalar_tensor_tensor(out=a[:], in0=t[:], scalar=1.0, in1=factor[:], op0=ALU.add, op1=ALU.mult)
            return a

        def reciprocal(name, t):
            a = column(name)
            nc.vector.reciprocal(out=a[:], in_=t[:])
            return a

        def line(name, t, scale, bias):
            a = column(name)
            nc.scalar.activation(out=a[:], in_=t[:], func=ACT.Identity, scale=scale, bias=bias)
            return a

        def negmax(name, n):
            a = column(name)
            nc.vector.tensor_reduce(out=a[:], in_=half_norm[:, 0:n], axis=AXIS.X, op=ALU.max, negate=True)
            return a

        def p_of(m, cut=slice(0, O)):
            return p_all[:, m, cut]

        def pair(name, a, b, op):
            r = column(name)
            nc.vector.tensor_tensor(out=r[:], in0=a[:], in1=b[:], op=op)
            return r

        d1, r1, d2, r2, u3, r3, uS, rS = [wide(n) for n in ("d1", "r1", "d2", "r2", "u3", "r3", "uS", "rS")]
        add_b2(3)
        root(half_norm[:, 1:2], 1, 2, both)
        t1 = tanh("t1", 0, half_norm[:, 1:2], -1.0)
        square(3)
        root(half_norm[:, 2:3], 2, 3, both)
        minus(d1[:], p_of(1), p_of(0))
        neg_max1 = negmax("neg_max1", 2)
        w1 = affine("w1", t1, 0.5, 0.5)
        add_b2(4)
        a1 = column("a1")
        nc.scalar.activation(out=a1[:], in_=t1[:], func=ACT.Abs)
        aa = line("aa", a1, 1.0, plus_one)
        am = line("am", a1, 1.0, minus_one)
        ap = line("ap", a1, 1.0, plus_three)
        t2 = tanh("t2", 2, neg_max1[:])
        square(4)
        store(nc.sync, 0, high, p_of(4))
        root(half_norm[:, 3:4], 3, 4, both)
        root(half_norm[:, 4:5], 4, 5, both)
        for cut in CUTS:
            weigh(r1[:, cut], d1[:, cut], w1, p_of(0, cut))
        neg_max2 = negmax("neg_max2", 3)
        den2 = affine("den2", t2, am[:], ap[:])
        num2 = plus_one_times("num2", t2, aa)
        abs2 = magnitude("abs2", t2)
        minus(d2[:, A], p_of(2, A), r1[:, A])
        rden2 = reciprocal("rden2", den2)
        a2 = plus_one_times("a2", abs2, aa)
        minus(d2[:, B], p_of(2, B), r1[:, B])
        w2 = pair("w2", num2, rden2, ALU.mult)
        am2 = pair("am2", a2, den2, ALU.subtract)
        ap2 = pair("ap2", a2, den2, ALU.add)
        t3 = tanh("t3", 3, neg_max2[:])
        tS = tanh("tS", 4, half_norm[:, 3:4], -1.0)
        vS = line("vS", tS, -0.5, half)
        wS = line("wS", tS, 0.5, half)
        for cut in CUTS:
            nc.scalar.activation(out=uS[:, cut], in_=p_of(4, cut), func=ACT.Copy, scale=vS[:])
        num3 = plus_one_times("num3", t3, a2)
        den3 = affine("den3", t3, am2[:], ap2[:])
        weigh(r2[:, A], d2[:, A], w2, r1[:, A])
        rden3 = reciprocal("rden3", den3)
        rest3 = pair("rest3", den3, num3, ALU.subtract)
        weigh(r2[:, B], d2[:, B], w2, r1[:, B])
        store(nc.sync, 2, low, r2)
        w3 = pair("w3", num3, rden3, ALU.mult)
        for cut in CUTS:
            nc.vector.tensor_scalar(
                out=u3[:, cut], in0=r2[:, cut], scalar1=rest3[:], scalar2=rden3[:], op0=ALU.mult, op1=ALU.mult
            )
        for cut in CUTS:
            weigh(r3[:, cut], p_of(3, cut), w3, u3[:, cut])
        store(nc.sync, 3, high, r3)
        for cut in CUTS:
            weigh(rS[:, cut], p_of(3, cut), wS, uS[:, cut])
        store(nc.scalar, 1, low, rS)
